import numpy as np
import ml_dtypes


def mxq(x, axis, fmt="e4m3"):
    dtype, down = {"e4m3": (ml_dtypes.float8_e4m3fn, 7), "e5m2": (ml_dtypes.float8_e5m2, 14)}[fmt]
    v = np.moveaxis(np.asarray(x, np.float32).astype(ml_dtypes.bfloat16).astype(np.float64), axis, -1)
    blocks = v.reshape(v.shape[:-1] + (-1, 32))
    amax = np.abs(blocks).max(-1, keepdims=True)
    byte = np.maximum(np.where(amax > 0, np.frexp(amax)[1] - 1 + 127, 0) - down, 1)
    scale = np.exp2(byte - 127.0)
    codes = (blocks / scale).astype(np.float32).astype(dtype).astype(np.float64)
    return np.moveaxis((codes * scale).reshape(v.shape), -1, axis)


WIDE = False


def mx_kscale(k):
    if not WIDE:
        return np.ones(k)
    levels = np.array([10, -10, 5, -5, 0])
    a = np.random.permutation(np.resize(levels, k // 512 * 4)).reshape(k // 512, 4)
    idx = np.arange(k)
    return np.exp2(a[idx // 512, idx % 128 // 32])


BF16 = ml_dtypes.bfloat16


def bf(x):
    return np.asarray(x, np.float32).astype(BF16)


def f64(x):
    return np.asarray(x).astype(np.float64)


B, S, H, D = 4, 1024, 4, 128
HD = H * D
LAYER_NUMBER = 2.0
NORM_FACTOR = LAYER_NUMBER * np.sqrt(D)


def setup_inputs():
    s = mx_kscale(HD)
    return {
        "hidden_states": bf(np.random.standard_normal((B, S, HD)) * s),
        "W_value": bf(np.random.standard_normal((HD, HD)) / np.sqrt(HD) / s[:, None]),
        "b_value": bf(np.random.standard_normal(HD) * 0.1),
        "query": bf(np.random.standard_normal((B, H, S, D))),
        "key": bf(np.random.standard_normal((B, H, S, D))),
        "alibi": bf(np.random.standard_normal((B, H, S))[:, :, None, :]),
        "attention_mask": bf(np.random.standard_normal((B, S, S))[:, None, :, :]),
    }


def reference(hidden_states, W_value, b_value, query, key, alibi, attention_mask):
    v = (mxq(f64(hidden_states), 2, "e4m3") @ mxq(f64(W_value), 0, "e4m3")) + f64(b_value)
    value = v.reshape(B, S, H, D).transpose(0, 2, 1, 3)
    scores = f64(query) @ f64(key).transpose(0, 1, 3, 2) / NORM_FACTOR
    scores = scores + f64(alibi) / LAYER_NUMBER
    scores = scores * LAYER_NUMBER + f64(attention_mask)
    e = np.exp(scores - scores.max(-1, keepdims=True))
    context = (mxq(e, 3, "e4m3") @ mxq(value, 2, "e4m3")) / e.sum(-1, keepdims=True)
    return context.transpose(0, 2, 1, 3).reshape(B, S, HD)

@@ -1,0 +1,326 @@
+import math
+from contextlib import ExitStack
+
+import concourse.mybir as mybir
+from concourse.masks import make_identity
+
+BF16 = mybir.dt.bfloat16
+F32 = mybir.dt.float32
+U32 = mybir.dt.uint32
+U8 = mybir.dt.uint8
+FP8X4 = mybir.dt.float8_e4m3fn_x4
+ALU = mybir.AluOpType
+ACT = mybir.ActivationFunctionType
+AXIS = mybir.AxisListType
+
+B, S, H, D = 4, 1024, 4, 128
+HD = H * D
+P = 128
+TILES = S // P
+BANK = 512
+K_PASS = 512
+PASSES = S // K_PASS
+ROWS = 4
+CHUNKS = TILES // ROWS
+AHEAD = 2
+SQRT_D = math.sqrt(D)
+
+FLOPS = 2 * B * S * HD * HD + 2 * 2 * B * H * S * S * D
+
+
+def interleave_out_of_psum(copy, grouped, planes):
+    copy(
+        out=grouped[:].rearrange("p (c u w) -> p c u w", u=2, w=2),
+        in_=planes[:].bitcast(BF16).rearrange("p (u c w) -> p c u w", u=2, w=2),
+    )
+
+
+def tile_fastbloomattention_pa_t_kernel(
+    tc, hidden_states, W_value, b_value, query, key, alibi, attention_mask, out
+):
+    nc = tc.nc
+    with ExitStack() as pools:
+        const = pools.enter_context(tc.tile_pool(name="const", bufs=1))
+        raw = pools.enter_context(tc.tile_pool(name="raw", bufs=1))
+        per_batch = pools.enter_context(tc.tile_pool(name="per_batch", bufs=2))
+        per_head = pools.enter_context(tc.tile_pool(name="per_head", bufs=2))
+        terms = pools.enter_context(tc.tile_pool(name="terms", bufs=AHEAD + 1))
+        stage = pools.enter_context(tc.tile_pool(name="stage", bufs=2))
+        rows = pools.enter_context(tc.tile_pool(name="rows", bufs=3))
+        outs = pools.enter_context(tc.tile_pool(name="outs", bufs=2))
+        psum_scores = pools.enter_context(tc.psum_pool(name="psum_scores", bufs=4))
+        psum_turn = pools.enter_context(tc.psum_pool(name="psum_turn", bufs=2))
+        psum_mx = pools.enter_context(tc.psum_pool(name="psum_mx", bufs=2))
+
+        ident_bf = const.tile([P, P], BF16)
+        make_identity(nc, ident_bf[:])
+        ident_f32 = const.tile([P, P], F32)
+        make_identity(nc, ident_f32[:])
+
+        def turn_queries_and_keys(b, h):
+            turned = []
+            for label, source in (("q", query), ("k", key)):
+                loaded = per_head.tile([P, TILES, D], BF16, name=label + "_raw")
+                nc.sync.dma_start(
+                    out=loaded[:], in_=source[b, h].rearrange("(t p) d -> p t d", p=P)
+                )
+                turned_ps = psum_turn.tile([P, S], BF16, tag="turn", name=label + "_ps")
+                for t in range(TILES):
+                    nc.tensor.transpose(
+                        turned_ps[:, t * P : (t + 1) * P], loaded[:, t, :], ident_bf[:]
+                    )
+                kept = per_head.tile([P, S], BF16, name=label + "T")
+                nc.scalar.copy(out=kept[:], in_=turned_ps[:])
+                turned.append(kept)
+            return turned
+
+        def load_batch(b):
+            mask_raw = raw.tile([P, TILES, S], BF16)
+            mask_rows = attention_mask[b, 0].rearrange("(t p) k -> p t k", p=P)
+            for c in range(CHUNKS):
+                its = slice(c * ROWS, (c + 1) * ROWS)
+                nc.sync.dma_start(out=mask_raw[:, its, :], in_=mask_rows[:, its, :])
+            hid_raw = raw.tile([P, 4 * 2 * HD], BF16)
+            nc.sync.dma_start(
+                out=hid_raw[:].rearrange("p (j c) -> p j c", j=4),
+                in_=hidden_states[b].rearrange("(j p w) c -> p j (w c)", j=4, w=2),
+            )
+            return mask_raw, hid_raw
+
+        def turn_mask(mask_raw):
+            maskT = per_batch.tile([P, TILES, S], BF16)
+            for c in range(CHUNKS):
+                for pair in range(TILES // 2):
+                    mask_ps = psum_turn.tile([P, 2 * BANK], BF16, tag="turn")
+                    for a in range(2):
+                        kt = 2 * pair + a
+                        for r in range(ROWS):
+                            spot = (a * ROWS + r) * P
+                            nc.tensor.transpose(
+                                mask_ps[:, spot : spot + P],
+                                mask_raw[:, c * ROWS + r, kt * P : (kt + 1) * P],
+                                ident_bf[:],
+                            )
+                    nc.vector.tensor_copy(
+                        out=maskT[:, 2 * pair : 2 * pair + 2, c * BANK : (c + 1) * BANK],
+                        in_=mask_ps[:].rearrange("p (a i) -> p a i", a=2),
+                    )
+            return maskT
+
+        def build_term(b, h, c, maskT):
+            term = terms.tile([P, TILES, BANK], F32)
+            for kt in range(TILES):
+                column = (b * H + h) * TILES + kt
+                nc.gpsimd.tensor_scalar(
+                    out=term[:, kt, :],
+                    in0=maskT[:, kt, c * BANK : (c + 1) * BANK],
+                    scalar1=SQRT_D,
+                    scalar2=alibi_cols[:, column : column + 1],
+                    op0=ALU.mult,
+                    op1=ALU.add,
+                )
+            return term
+
+        def project_values(hid_raw):
+            hid_words = hid_raw[:].bitcast(F32).rearrange("p (j w x) -> p j w x", j=4, w=2)
+            h_codes = stage.tile([P, 4 * 2 * P], U32, align_bytes=64)
+            h_scales = stage.tile([P, 4 * 2 * P], U8, align_bytes=64)
+            for j in range(4):
+                hid_ps = psum_turn.tile([P, BANK], F32, tag="turn")
+                for u in range(2):
+                    for w in range(2):
+                        spot = (u * 2 + w) * P
+                        nc.tensor.transpose(
+                            hid_ps[:, spot : spot + P],
+                            hid_words[:, j, w, u * P : (u + 1) * P],
+                            ident_f32[:],
+                        )
+                h_grp = stage.tile([P, 2 * P * 4], BF16, align_bytes=64)
+                interleave_out_of_psum(nc.vector.tensor_copy, h_grp, hid_ps)
+                block = slice(j * 2 * P, (j + 1) * 2 * P)
+                nc.vector.quantize_mx(
+                    out=h_codes[:, block].bitcast(FP8X4), scales=h_scales[:, block], in_=h_grp[:]
+                )
+            v_codes = per_batch.tile([P, PASSES * HD], U32, align_bytes=64)
+            v_scales = per_batch.tile([P, PASSES * HD], U8, align_bytes=64)
+            for g in range(PASSES):
+                v_grp = stage.tile([P, HD * 4], BF16, align_bytes=64)
+                for h in range(H):
+                    head = slice(h * D, (h + 1) * D)
+                    v_ps = psum_mx.tile([P, BANK], F32, tag="mx")
+                    for t in range(4):
+                        keys = slice((4 * g + t) * P, (4 * g + t + 1) * P)
+                        nc.tensor.matmul_mx(
+                            out=v_ps[:, t * D : (t + 1) * D],
+                            lhsT=h_codes[:, keys].bitcast(FP8X4),
+                            lhsT_scale=h_scales[:, keys],
+                            rhs=w_codes[:, head].bitcast(FP8X4),
+                            rhs_scale=w_scales[:, head],
+                            start=True,
+                            stop=True,
+                        )
+                    nc.vector.tensor_tensor(
+                        out=v_grp[:, h * D * 4 : (h + 1) * D * 4].rearrange(
+                            "p (d t) -> p d t", t=4
+                        ),
+                        in0=v_ps[:].rearrange("p (t d) -> p d t", t=4),
+                        in1=bias_bc[:, head].unsqueeze(2).to_broadcast([P, D, 4]),
+                        op=ALU.add,
+                    )
+                one_pass = slice(g * HD, (g + 1) * HD)
+                nc.vector.quantize_mx(
+                    out=v_codes[:, one_pass].bitcast(FP8X4),
+                    scales=v_scales[:, one_pass],
+                    in_=v_grp[:],
+                )
+            return v_codes, v_scales
+
+        def attend(b, h, c, qT, kT, term, v_codes, v_scales):
+            ctx_ps = psum_mx.tile([P, BANK], F32, tag="mx")
+            part_sums = outs.tile([P, ROWS, 2], F32)
+            for r in range(ROWS):
+                queries = slice((c * ROWS + r) * P, (c * ROWS + r + 1) * P)
+                tops = rows.tile([P, 2], F32)
+                halves = []
+                for half in range(2):
+                    scores = psum_scores.tile([P, BANK], F32, tag="scores")
+                    nc.tensor.matmul(
+                        scores[:],
+                        lhsT=qT[:, queries],
+                        rhs=kT[:, half * BANK : (half + 1) * BANK],
+                        start=True,
+                        stop=False,
+                    )
+                    for a in range(4):
+                        nc.tensor.matmul(
+                            scores[:, a * P : (a + 1) * P],
+                            lhsT=term[:, 4 * half + a, r * P : (r + 1) * P],
+                            rhs=ident_f32[:],
+                            start=False,
+                            stop=(a == 3),
+                            is_transpose=True,
+                        )
+                    nc.vector.tensor_reduce(
+                        out=tops[:, half : half + 1], in_=scores[:], axis=AXIS.X, op=ALU.max
+                    )
+                    halves.append(scores)
+                shift = rows.tile([P, 1], F32)
+                nc.vector.tensor_scalar(
+                    out=shift[:],
+                    in0=tops[:, 0:1],
+                    scalar1=tops[:, 1:2],
+                    scalar2=-1.0 / SQRT_D,
+                    op0=ALU.max,
+                    op1=ALU.mult,
+                )
+                e = rows.tile([P, S], BF16)
+                for half in range(2):
+                    nc.scalar.activation(
+                        out=e[:, half * BANK : (half + 1) * BANK],
+                        in_=halves[half][:],
+                        func=ACT.Exp,
+                        bias=shift[:],
+                        scale=1.0 / SQRT_D,
+                        accum_out=part_sums[:, r, half : half + 1],
+                    )
+                e_words = e[:].bitcast(F32)
+                eT_ps = psum_turn.tile([P, BANK], F32, tag="turn")
+                for g in range(PASSES):
+                    for u in range(2):
+                        nc.tensor.transpose(
+                            eT_ps[:, (u * PASSES + g) * P : (u * PASSES + g + 1) * P],
+                            e_words[:, (2 * g + u) * P : (2 * g + u + 1) * P],
+                            ident_f32[:],
+                        )
+                e_grp = rows.tile([P, S], BF16, align_bytes=64)
+                interleave_out_of_psum(nc.scalar.copy, e_grp, eT_ps)
+                e_codes = rows.tile([P, PASSES * P], U32, align_bytes=64)
+                e_scales = rows.tile([P, PASSES * P], U8, align_bytes=64)
+                nc.vector.quantize_mx(
+                    out=e_codes[:].bitcast(FP8X4), scales=e_scales[:], in_=e_grp[:]
+                )
+                for g in range(PASSES):
+                    mine = slice(g * P, (g + 1) * P)
+                    theirs = slice(g * HD + h * D, g * HD + (h + 1) * D)
+                    nc.tensor.matmul_mx(
+                        out=ctx_ps[:, r * D : (r + 1) * D],
+                        lhsT=e_codes[:, mine].bitcast(FP8X4),
+                        lhsT_scale=e_scales[:, mine],
+                        rhs=v_codes[:, theirs].bitcast(FP8X4),
+                        rhs_scale=v_scales[:, theirs],
+                        start=(g == 0),
+                        stop=(g == PASSES - 1),
+                    )
+            sums = outs.tile([P, ROWS], F32)
+            nc.vector.tensor_reduce(out=sums[:], in_=part_sums[:], axis=AXIS.X, op=ALU.add)
+            inverse = outs.tile([P, ROWS], F32)
+            nc.vector.reciprocal(out=inverse[:], in_=sums[:])
+            context = outs.tile([P, ROWS, D], F32)
+            nc.vector.tensor_tensor(
+                out=context[:],
+                in0=ctx_ps[:].rearrange("p (r d) -> p r d", r=ROWS),
+                in1=inverse[:].unsqueeze(2).to_broadcast([P, ROWS, D]),
+                op=ALU.mult,
+            )
+            nc.sync.dma_start(
+                out=out[b].rearrange("(t p) x -> p t x", p=P)[
+                    :, c * ROWS : (c + 1) * ROWS, h * D : (h + 1) * D
+                ],
+                in_=context[:],
+            )
+
+        alibi_rows = const.tile([P, P], BF16)
+        nc.sync.dma_start(
+            out=alibi_rows[:], in_=alibi.rearrange("b h o (t k) -> (b h o t) k", k=P)
+        )
+        alibi_ps = psum_turn.tile([P, P], BF16, tag="turn")
+        nc.tensor.transpose(alibi_ps[:], alibi_rows[:], ident_bf[:])
+        alibi_cols = const.tile([P, P], F32)
+        nc.vector.tensor_scalar(
+            out=alibi_cols[:], in0=alibi_ps[:], scalar1=SQRT_D, scalar2=None, op0=ALU.mult
+        )
+
+        heads = [(b, h) for b in range(B) for h in range(H)]
+        chunks = [(b, h, c) for (b, h) in heads for c in range(CHUNKS)]
+        turned_of = {heads[0]: turn_queries_and_keys(0, 0)}
+        raw_of = {0: load_batch(0)}
+        maskT_of = {0: turn_mask(raw_of[0][0])}
+        term_of = {}
+        for first in chunks[:AHEAD]:
+            term_of[first] = build_term(first[0], first[1], first[2], maskT_of[0])
+
+        w_raw = const.tile([P, 4, HD], BF16)
+        nc.sync.dma_start(
+            out=w_raw[:].rearrange("p (u w) x -> p u (w x)", u=2),
+            in_=W_value.rearrange("(u p w) x -> p u (w x)", u=2, w=2),
+        )
+        bias_bc = const.tile([P, HD], BF16)
+        nc.sync.dma_start(out=bias_bc[:], in_=b_value.partition_broadcast(P))
+        w_grp = const.tile([P, HD, 4], BF16, align_bytes=64)
+        nc.vector.tensor_copy(out=w_grp[:], in_=w_raw[:].rearrange("p t x -> p x t"))
+        w_codes = const.tile([P, HD], U32, align_bytes=64)
+        w_scales = const.tile([P, HD], U8, align_bytes=64)
+        nc.vector.quantize_mx(
+            out=w_codes[:].bitcast(FP8X4),
+            scales=w_scales[:],
+            in_=w_grp[:].rearrange("p x t -> p (x t)"),
+        )
+        values_of = {0: project_values(raw_of[0][1])}
+
+        for n, (b, h, c) in enumerate(chunks):
+            if c == 0 and heads.index((b, h)) + 1 < len(heads):
+                following = heads[heads.index((b, h)) + 1]
+                turned_of[following] = turn_queries_and_keys(following[0], following[1])
+            if c == 0 and b + 1 < B:
+                if h == 0:
+                    raw_of[b + 1] = load_batch(b + 1)
+                if h == 1:
+                    values_of[b + 1] = project_values(raw_of[b + 1][1])
+                if h == 2:
+                    maskT_of[b + 1] = turn_mask(raw_of[b + 1][0])
+            if n + AHEAD < len(chunks):
+                later = chunks[n + AHEAD]
+                term_of[later] = build_term(later[0], later[1], later[2], maskT_of[later[0]])
+            qT, kT = turned_of[(b, h)]
+            v_codes, v_scales = values_of[b]
+            attend(b, h, c, qT, kT, term_of[(b, h, c)], v_codes, v_scales)

@@ -22,6 +22,8 @@ K_PASS = 512
 PASSES = S // K_PASS
 ROWS = 4
 CHUNKS = TILES // ROWS
+ALL_ROWS = B * H * TILES
+ALL_CHUNKS = ALL_ROWS // ROWS
 AHEAD = 2
 SQRT_D = math.sqrt(D)
 
@@ -46,204 +48,266 @@ def tile_fastbloomattention_pa_t_kernel(
         per_head = pools.enter_context(tc.tile_pool(name="per_head", bufs=2))
         terms = pools.enter_context(tc.tile_pool(name="terms", bufs=AHEAD + 1))
         stage = pools.enter_context(tc.tile_pool(name="stage", bufs=2))
-        rows = pools.enter_context(tc.tile_pool(name="rows", bufs=3))
-        outs = pools.enter_context(tc.tile_pool(name="outs", bufs=2))
+        per_row = pools.enter_context(tc.tile_pool(name="per_row", bufs=3))
+        per_chunk = pools.enter_context(tc.tile_pool(name="per_chunk", bufs=3))
         psum_scores = pools.enter_context(tc.psum_pool(name="psum_scores", bufs=4))
-        psum_turn = pools.enter_context(tc.psum_pool(name="psum_turn", bufs=2))
-        psum_mx = pools.enter_context(tc.psum_pool(name="psum_mx", bufs=2))
+        psum_turn = pools.enter_context(tc.psum_pool(name="psum_turn", bufs=3))
+        psum_mx = pools.enter_context(tc.psum_pool(name="psum_mx", bufs=1))
 
         ident_bf = const.tile([P, P], BF16)
         make_identity(nc, ident_bf[:])
         ident_f32 = const.tile([P, P], F32)
         make_identity(nc, ident_f32[:])
+        pools.enter_context(tc.manual_schedule())
 
-        def turn_queries_and_keys(b, h):
-            turned = []
+        qk_raw, qk_turned = {}, {}
+        mask_raw, maskT, hid_raw = {}, {}, {}
+        h_quantised, v_grouped, v_quantised = {}, {}, {}
+        term, scores, tops, shift, e, eT, e_grouped = {}, {}, {}, {}, {}, {}, {}
+        e_quantised, part_sums, context_ps = {}, {}, {}
+
+        def load_queries_and_keys(n):
             for label, source in (("q", query), ("k", key)):
                 loaded = per_head.tile([P, TILES, D], BF16, name=label + "_raw")
                 nc.sync.dma_start(
-                    out=loaded[:], in_=source[b, h].rearrange("(t p) d -> p t d", p=P)
+                    out=loaded[:], in_=source[n // H, n % H].rearrange("(t p) d -> p t d", p=P)
                 )
-                turned_ps = psum_turn.tile([P, S], BF16, tag="turn", name=label + "_ps")
-                for t in range(TILES):
-                    nc.tensor.transpose(
-                        turned_ps[:, t * P : (t + 1) * P], loaded[:, t, :], ident_bf[:]
-                    )
-                kept = per_head.tile([P, S], BF16, name=label + "T")
-                nc.scalar.copy(out=kept[:], in_=turned_ps[:])
-                turned.append(kept)
-            return turned
+                qk_raw[(label, n)] = loaded
 
-        def load_batch(b):
-            mask_raw = raw.tile([P, TILES, S], BF16)
+        def turn_queries_or_keys(label, n):
+            turned_ps = psum_turn.tile([P, S], BF16, tag="turn", name=label + "_ps")
+            for t in range(TILES):
+                nc.tensor.transpose(
+                    turned_ps[:, t * P : (t + 1) * P], qk_raw[(label, n)][:, t, :], ident_bf[:]
+                )
+            kept = per_head.tile([P, S], BF16, name=label + "T")
+            nc.scalar.copy(out=kept[:], in_=turned_ps[:])
+            qk_turned[(label, n)] = kept
+
+        def load_mask(b):
+            loaded = raw.tile([P, TILES, S], BF16, name="mask_raw")
             mask_rows = attention_mask[b, 0].rearrange("(t p) k -> p t k", p=P)
             for c in range(CHUNKS):
                 its = slice(c * ROWS, (c + 1) * ROWS)
-                nc.sync.dma_start(out=mask_raw[:, its, :], in_=mask_rows[:, its, :])
-            hid_raw = raw.tile([P, 4 * 2 * HD], BF16)
-            nc.sync.dma_start(
-                out=hid_raw[:].rearrange("p (j c) -> p j c", j=4),
-                in_=hidden_states[b].rearrange("(j p w) c -> p j (w c)", j=4, w=2),
-            )
-            return mask_raw, hid_raw
+                nc.sync.dma_start(out=loaded[:, its, :], in_=mask_rows[:, its, :])
+            mask_raw[b] = loaded
 
-        def turn_mask(mask_raw):
-            maskT = per_batch.tile([P, TILES, S], BF16)
-            for c in range(CHUNKS):
-                for pair in range(TILES // 2):
-                    mask_ps = psum_turn.tile([P, 2 * BANK], BF16, tag="turn")
-                    for a in range(2):
-                        kt = 2 * pair + a
-                        for r in range(ROWS):
-                            spot = (a * ROWS + r) * P
-                            nc.tensor.transpose(
-                                mask_ps[:, spot : spot + P],
-                                mask_raw[:, c * ROWS + r, kt * P : (kt + 1) * P],
-                                ident_bf[:],
-                            )
-                    nc.vector.tensor_copy(
-                        out=maskT[:, 2 * pair : 2 * pair + 2, c * BANK : (c + 1) * BANK],
-                        in_=mask_ps[:].rearrange("p (a i) -> p a i", a=2),
+        def turn_mask(b, piece):
+            c, pair = piece // 4, piece % 4
+            if piece == 0:
+                maskT[b] = per_batch.tile([P, TILES, S], BF16, name="maskT")
+            mask_ps = psum_turn.tile([P, 2 * BANK], BF16, tag="turn")
+            for a in range(2):
+                kt = 2 * pair + a
+                for r in range(ROWS):
+                    spot = (a * ROWS + r) * P
+                    nc.tensor.transpose(
+                        mask_ps[:, spot : spot + P],
+                        mask_raw[b][:, c * ROWS + r, kt * P : (kt + 1) * P],
+                        ident_bf[:],
                     )
-            return maskT
+            nc.vector.tensor_copy(
+                out=maskT[b][:, 2 * pair : 2 * pair + 2, c * BANK : (c + 1) * BANK],
+                in_=mask_ps[:].rearrange("p (a i) -> p a i", a=2),
+            )
 
-        def build_term(b, h, c, maskT):
-            term = terms.tile([P, TILES, BANK], F32)
+        def build_term(n):
+            head, c = n // CHUNKS, n % CHUNKS
+            built = terms.tile([P, TILES, BANK], F32, name="term")
             for kt in range(TILES):
-                column = (b * H + h) * TILES + kt
+                column = head * TILES + kt
                 nc.gpsimd.tensor_scalar(
-                    out=term[:, kt, :],
-                    in0=maskT[:, kt, c * BANK : (c + 1) * BANK],
+                    out=built[:, kt, :],
+                    in0=maskT[head // H][:, kt, c * BANK : (c + 1) * BANK],
                     scalar1=SQRT_D,
                     scalar2=alibi_cols[:, column : column + 1],
                     op0=ALU.mult,
                     op1=ALU.add,
                 )
-            return term
+            term[n] = built
 
-        def project_values(hid_raw):
-            hid_words = hid_raw[:].bitcast(F32).rearrange("p (j w x) -> p j w x", j=4, w=2)
-            h_codes = stage.tile([P, 4 * 2 * P], U32, align_bytes=64)
-            h_scales = stage.tile([P, 4 * 2 * P], U8, align_bytes=64)
-            for j in range(4):
-                hid_ps = psum_turn.tile([P, BANK], F32, tag="turn")
-                for u in range(2):
-                    for w in range(2):
-                        spot = (u * 2 + w) * P
-                        nc.tensor.transpose(
-                            hid_ps[:, spot : spot + P],
-                            hid_words[:, j, w, u * P : (u + 1) * P],
-                            ident_f32[:],
-                        )
-                h_grp = stage.tile([P, 2 * P * 4], BF16, align_bytes=64)
-                interleave_out_of_psum(nc.vector.tensor_copy, h_grp, hid_ps)
-                block = slice(j * 2 * P, (j + 1) * 2 * P)
-                nc.vector.quantize_mx(
-                    out=h_codes[:, block].bitcast(FP8X4), scales=h_scales[:, block], in_=h_grp[:]
+        def load_hidden(b):
+            loaded = raw.tile([P, 4 * 2 * HD], BF16, name="hid_raw")
+            nc.sync.dma_start(
+                out=loaded[:].rearrange("p (j c) -> p j c", j=4),
+                in_=hidden_states[b].rearrange("(j p w) c -> p j (w c)", j=4, w=2),
+            )
+            hid_raw[b] = loaded
+
+        def quantise_hidden(b, j):
+            if j == 0:
+                h_quantised[b] = (
+                    stage.tile([P, 4 * 2 * P], U32, align_bytes=64, name="h_codes"),
+                    stage.tile([P, 4 * 2 * P], U8, align_bytes=64, name="h_scales"),
                 )
-            v_codes = per_batch.tile([P, PASSES * HD], U32, align_bytes=64)
-            v_scales = per_batch.tile([P, PASSES * HD], U8, align_bytes=64)
-            for g in range(PASSES):
-                v_grp = stage.tile([P, HD * 4], BF16, align_bytes=64)
-                for h in range(H):
-                    head = slice(h * D, (h + 1) * D)
-                    v_ps = psum_mx.tile([P, BANK], F32, tag="mx")
-                    for t in range(4):
-                        keys = slice((4 * g + t) * P, (4 * g + t + 1) * P)
-                        nc.tensor.matmul_mx(
-                            out=v_ps[:, t * D : (t + 1) * D],
-                            lhsT=h_codes[:, keys].bitcast(FP8X4),
-                            lhsT_scale=h_scales[:, keys],
-                            rhs=w_codes[:, head].bitcast(FP8X4),
-                            rhs_scale=w_scales[:, head],
-                            start=True,
-                            stop=True,
-                        )
-                    nc.vector.tensor_tensor(
-                        out=v_grp[:, h * D * 4 : (h + 1) * D * 4].rearrange(
-                            "p (d t) -> p d t", t=4
-                        ),
-                        in0=v_ps[:].rearrange("p (t d) -> p d t", t=4),
-                        in1=bias_bc[:, head].unsqueeze(2).to_broadcast([P, D, 4]),
-                        op=ALU.add,
+            h_codes, h_scales = h_quantised[b]
+            hid_words = hid_raw[b][:].bitcast(F32).rearrange("p (j w x) -> p j w x", j=4, w=2)
+            hid_ps = psum_turn.tile([P, BANK], F32, tag="turn")
+            for u in range(2):
+                for w in range(2):
+                    spot = (u * 2 + w) * P
+                    nc.tensor.transpose(
+                        hid_ps[:, spot : spot + P],
+                        hid_words[:, j, w, u * P : (u + 1) * P],
+                        ident_f32[:],
                     )
+            h_grp = stage.tile([P, 2 * P * 4], BF16, align_bytes=64)
+            interleave_out_of_psum(nc.vector.tensor_copy, h_grp, hid_ps)
+            block = slice(j * 2 * P, (j + 1) * 2 * P)
+            nc.vector.quantize_mx(
+                out=h_codes[:, block].bitcast(FP8X4), scales=h_scales[:, block], in_=h_grp[:]
+            )
+
+        def project_values(b, g, h):
+            if (g, h) == (0, 0):
+                v_quantised[b] = (
+                    per_batch.tile([P, PASSES * HD], U32, align_bytes=64, name="v_codes"),
+                    per_batch.tile([P, PASSES * HD], U8, align_bytes=64, name="v_scales"),
+                )
+            if h == 0:
+                v_grouped[b] = stage.tile([P, HD * 4], BF16, align_bytes=64, name="v_grp")
+            h_codes, h_scales = h_quantised[b]
+            head = slice(h * D, (h + 1) * D)
+            v_ps = psum_mx.tile([P, BANK], F32, tag="mx")
+            for t in range(4):
+                keys = slice((4 * g + t) * P, (4 * g + t + 1) * P)
+                nc.tensor.matmul_mx(
+                    out=v_ps[:, t * D : (t + 1) * D],
+                    lhsT=h_codes[:, keys].bitcast(FP8X4),
+                    lhsT_scale=h_scales[:, keys],
+                    rhs=w_codes[:, head].bitcast(FP8X4),
+                    rhs_scale=w_scales[:, head],
+                    start=True,
+                    stop=True,
+                )
+            nc.vector.tensor_tensor(
+                out=v_grouped[b][:, h * D * 4 : (h + 1) * D * 4].rearrange("p (d t) -> p d t", t=4),
+                in0=v_ps[:].rearrange("p (t d) -> p d t", t=4),
+                in1=bias_bc[:, head].unsqueeze(2).to_broadcast([P, D, 4]),
+                op=ALU.add,
+            )
+            if h == H - 1:
+                v_codes, v_scales = v_quantised[b]
                 one_pass = slice(g * HD, (g + 1) * HD)
                 nc.vector.quantize_mx(
                     out=v_codes[:, one_pass].bitcast(FP8X4),
                     scales=v_scales[:, one_pass],
-                    in_=v_grp[:],
+                    in_=v_grouped[b][:],
                 )
-            return v_codes, v_scales
 
-        def attend(b, h, c, qT, kT, term, v_codes, v_scales):
-            ctx_ps = psum_mx.tile([P, BANK], F32, tag="mx")
-            part_sums = outs.tile([P, ROWS, 2], F32)
+        def prepare(n, i):
+            b, h = n // H, n % H
+            if i < 2 and n + 1 < B * H:
+                turn_queries_or_keys("qk"[i], n + 1)
+            if i == 2 and n + 2 < B * H:
+                load_queries_and_keys(n + 2)
+            if i < 2 or b + 1 >= B:
+                return
+            if h < 2 and i < 6:
+                turn_mask(b + 1, 4 * h + i - 2)
+            if h == 1 and i == 6 and b + 2 < B:
+                load_mask(b + 2)
+            if h >= 2 and i < 4:
+                quantise_hidden(b + 1, 2 * (h - 2) + i - 2)
+            if h >= 2 and i >= 4:
+                project_values(b + 1, h - 2, i - 4)
+            if h == 3 and i == 7 and b + 2 < B:
+                load_hidden(b + 2)
+
+        def fill_scores(k, half):
+            n, r = k // ROWS, k % ROWS
+            queries = slice((k % TILES) * P, (k % TILES + 1) * P)
+            if half == 0:
+                tops[k] = per_row.tile([P, 2], F32, name="tops")
+            bank = psum_scores.tile([P, BANK], F32, tag="scores")
+            nc.tensor.matmul(
+                bank[:],
+                lhsT=qk_turned[("q", k // TILES)][:, queries],
+                rhs=qk_turned[("k", k // TILES)][:, half * BANK : (half + 1) * BANK],
+                start=True,
+                stop=False,
+            )
+            for a in range(4):
+                nc.tensor.matmul(
+                    bank[:, a * P : (a + 1) * P],
+                    lhsT=term[n][:, 4 * half + a, r * P : (r + 1) * P],
+                    rhs=ident_f32[:],
+                    start=False,
+                    stop=(a == 3),
+                    is_transpose=True,
+                )
+            nc.vector.tensor_reduce(
+                out=tops[k][:, half : half + 1], in_=bank[:], axis=AXIS.X, op=ALU.max
+            )
+            scores[(k, half)] = bank
+
+        def find_shift(k):
+            shift[k] = per_row.tile([P, 1], F32, name="shift")
+            nc.vector.tensor_scalar(
+                out=shift[k][:],
+                in0=tops[k][:, 0:1],
+                scalar1=tops[k][:, 1:2],
+                scalar2=-1.0 / SQRT_D,
+                op0=ALU.max,
+                op1=ALU.mult,
+            )
+
+        def exponentials(k):
+            n, r = k // ROWS, k % ROWS
+            if r == 0:
+                part_sums[n] = per_chunk.tile([P, ROWS, 2], F32, name="part_sums")
+            e[k] = per_row.tile([P, S], BF16, name="e")
+            for half in range(2):
+                nc.scalar.activation(
+                    out=e[k][:, half * BANK : (half + 1) * BANK],
+                    in_=scores[(k, half)][:],
+                    func=ACT.Exp,
+                    bias=shift[k][:],
+                    scale=1.0 / SQRT_D,
+                    accum_out=part_sums[n][:, r, half : half + 1],
+                )
+
+        def turn_e(k):
+            e_words = e[k][:].bitcast(F32)
+            eT[k] = psum_turn.tile([P, BANK], F32, tag="turn", name="eT_ps")
+            for g in range(PASSES):
+                for u in range(2):
+                    nc.tensor.transpose(
+                        eT[k][:, (u * PASSES + g) * P : (u * PASSES + g + 1) * P],
+                        e_words[:, (2 * g + u) * P : (2 * g + u + 1) * P],
+                        ident_f32[:],
+                    )
+
+        def group_e(k):
+            e_grouped[k] = per_row.tile([P, S], BF16, align_bytes=64, name="e_grp")
+            interleave_out_of_psum(nc.scalar.copy, e_grouped[k], eT[k])
+
+        def quantise_e(k):
+            n, r = k // ROWS, k % ROWS
+            if r == 0:
+                e_quantised[n] = (
+                    per_chunk.tile([P, ROWS * PASSES * P], U32, align_bytes=64, name="e_codes"),
+                    per_chunk.tile([P, ROWS * PASSES * P], U8, align_bytes=64, name="e_scales"),
+                )
+            e_codes, e_scales = e_quantised[n]
+            mine = slice(r * PASSES * P, (r + 1) * PASSES * P)
+            nc.vector.quantize_mx(
+                out=e_codes[:, mine].bitcast(FP8X4),
+                scales=e_scales[:, mine],
+                in_=e_grouped[k][:],
+            )
+
+        def weigh_values(n):
+            b, h = n // (H * CHUNKS), (n // CHUNKS) % H
+            e_codes, e_scales = e_quantised[n]
+            v_codes, v_scales = v_quantised[b]
+            context_ps[n] = psum_mx.tile([P, BANK], F32, tag="mx", name="context_ps")
             for r in range(ROWS):
-                queries = slice((c * ROWS + r) * P, (c * ROWS + r + 1) * P)
-                tops = rows.tile([P, 2], F32)
-                halves = []
-                for half in range(2):
-                    scores = psum_scores.tile([P, BANK], F32, tag="scores")
-                    nc.tensor.matmul(
-                        scores[:],
-                        lhsT=qT[:, queries],
-                        rhs=kT[:, half * BANK : (half + 1) * BANK],
-                        start=True,
-                        stop=False,
-                    )
-                    for a in range(4):
-                        nc.tensor.matmul(
-                            scores[:, a * P : (a + 1) * P],
-                            lhsT=term[:, 4 * half + a, r * P : (r + 1) * P],
-                            rhs=ident_f32[:],
-                            start=False,
-                            stop=(a == 3),
-                            is_transpose=True,
-                        )
-                    nc.vector.tensor_reduce(
-                        out=tops[:, half : half + 1], in_=scores[:], axis=AXIS.X, op=ALU.max
-                    )
-                    halves.append(scores)
-                shift = rows.tile([P, 1], F32)
-                nc.vector.tensor_scalar(
-                    out=shift[:],
-                    in0=tops[:, 0:1],
-                    scalar1=tops[:, 1:2],
-                    scalar2=-1.0 / SQRT_D,
-                    op0=ALU.max,
-                    op1=ALU.mult,
-                )
-                e = rows.tile([P, S], BF16)
-                for half in range(2):
-                    nc.scalar.activation(
-                        out=e[:, half * BANK : (half + 1) * BANK],
-                        in_=halves[half][:],
-                        func=ACT.Exp,
-                        bias=shift[:],
-                        scale=1.0 / SQRT_D,
-                        accum_out=part_sums[:, r, half : half + 1],
-                    )
-                e_words = e[:].bitcast(F32)
-                eT_ps = psum_turn.tile([P, BANK], F32, tag="turn")
                 for g in range(PASSES):
-                    for u in range(2):
-                        nc.tensor.transpose(
-                            eT_ps[:, (u * PASSES + g) * P : (u * PASSES + g + 1) * P],
-                            e_words[:, (2 * g + u) * P : (2 * g + u + 1) * P],
-                            ident_f32[:],
-                        )
-                e_grp = rows.tile([P, S], BF16, align_bytes=64)
-                interleave_out_of_psum(nc.scalar.copy, e_grp, eT_ps)
-                e_codes = rows.tile([P, PASSES * P], U32, align_bytes=64)
-                e_scales = rows.tile([P, PASSES * P], U8, align_bytes=64)
-                nc.vector.quantize_mx(
-                    out=e_codes[:].bitcast(FP8X4), scales=e_scales[:], in_=e_grp[:]
-                )
-                for g in range(PASSES):
-                    mine = slice(g * P, (g + 1) * P)
+                    mine = slice((r * PASSES + g) * P, (r * PASSES + g + 1) * P)
                     theirs = slice(g * HD + h * D, g * HD + (h + 1) * D)
                     nc.tensor.matmul_mx(
-                        out=ctx_ps[:, r * D : (r + 1) * D],
+                        out=context_ps[n][:, r * D : (r + 1) * D],
                         lhsT=e_codes[:, mine].bitcast(FP8X4),
                         lhsT_scale=e_scales[:, mine],
                         rhs=v_codes[:, theirs].bitcast(FP8X4),
@@ -251,14 +315,17 @@ def tile_fastbloomattention_pa_t_kernel(
                         start=(g == 0),
                         stop=(g == PASSES - 1),
                     )
-            sums = outs.tile([P, ROWS], F32)
-            nc.vector.tensor_reduce(out=sums[:], in_=part_sums[:], axis=AXIS.X, op=ALU.add)
-            inverse = outs.tile([P, ROWS], F32)
+
+        def finish(n):
+            b, h, c = n // (H * CHUNKS), (n // CHUNKS) % H, n % CHUNKS
+            sums = per_chunk.tile([P, ROWS], F32)
+            nc.vector.tensor_reduce(out=sums[:], in_=part_sums[n][:], axis=AXIS.X, op=ALU.add)
+            inverse = per_chunk.tile([P, ROWS], F32)
             nc.vector.reciprocal(out=inverse[:], in_=sums[:])
-            context = outs.tile([P, ROWS, D], F32)
+            context = per_chunk.tile([P, ROWS, D], F32)
             nc.vector.tensor_tensor(
                 out=context[:],
-                in0=ctx_ps[:].rearrange("p (r d) -> p r d", r=ROWS),
+                in0=context_ps[n][:].rearrange("p (r d) -> p r d", r=ROWS),
                 in1=inverse[:].unsqueeze(2).to_broadcast([P, ROWS, D]),
                 op=ALU.mult,
             )
@@ -273,22 +340,8 @@ def tile_fastbloomattention_pa_t_kernel(
         nc.sync.dma_start(
             out=alibi_rows[:], in_=alibi.rearrange("b h o (t k) -> (b h o t) k", k=P)
         )
-        alibi_ps = psum_turn.tile([P, P], BF16, tag="turn")
-        nc.tensor.transpose(alibi_ps[:], alibi_rows[:], ident_bf[:])
-        alibi_cols = const.tile([P, P], F32)
-        nc.vector.tensor_scalar(
-            out=alibi_cols[:], in0=alibi_ps[:], scalar1=SQRT_D, scalar2=None, op0=ALU.mult
-        )
-
-        heads = [(b, h) for b in range(B) for h in range(H)]
-        chunks = [(b, h, c) for (b, h) in heads for c in range(CHUNKS)]
-        turned_of = {heads[0]: turn_queries_and_keys(0, 0)}
-        raw_of = {0: load_batch(0)}
-        maskT_of = {0: turn_mask(raw_of[0][0])}
-        term_of = {}
-        for first in chunks[:AHEAD]:
-            term_of[first] = build_term(first[0], first[1], first[2], maskT_of[0])
-
+        load_queries_and_keys(0)
+        load_mask(0)
         w_raw = const.tile([P, 4, HD], BF16)
         nc.sync.dma_start(
             out=w_raw[:].rearrange("p (u w) x -> p u (w x)", u=2),
@@ -296,6 +349,22 @@ def tile_fastbloomattention_pa_t_kernel(
         )
         bias_bc = const.tile([P, HD], BF16)
         nc.sync.dma_start(out=bias_bc[:], in_=b_value.partition_broadcast(P))
+        load_hidden(0)
+        load_queries_and_keys(1)
+
+        alibi_ps = psum_turn.tile([P, P], BF16, tag="turn")
+        nc.tensor.transpose(alibi_ps[:], alibi_rows[:], ident_bf[:])
+        alibi_cols = const.tile([P, P], F32)
+        nc.vector.tensor_scalar(
+            out=alibi_cols[:], in0=alibi_ps[:], scalar1=SQRT_D, scalar2=None, op0=ALU.mult
+        )
+        turn_queries_or_keys("q", 0)
+        turn_queries_or_keys("k", 0)
+        for c in range(CHUNKS):
+            for pair in range(4):
+                turn_mask(0, 4 * c + pair)
+            build_term(c)
+        load_mask(1)
         w_grp = const.tile([P, HD, 4], BF16, align_bytes=64)
         nc.vector.tensor_copy(out=w_grp[:], in_=w_raw[:].rearrange("p t x -> p x t"))
         w_codes = const.tile([P, HD], U32, align_bytes=64)
@@ -305,22 +374,32 @@ def tile_fastbloomattention_pa_t_kernel(
             scales=w_scales[:],
             in_=w_grp[:].rearrange("p x t -> p (x t)"),
         )
-        values_of = {0: project_values(raw_of[0][1])}
+        for j in range(4):
+            quantise_hidden(0, j)
+        load_hidden(1)
+        for g in range(PASSES):
+            for h in range(H):
+                project_values(0, g, h)
 
-        for n, (b, h, c) in enumerate(chunks):
-            if c == 0 and heads.index((b, h)) + 1 < len(heads):
-                following = heads[heads.index((b, h)) + 1]
-                turned_of[following] = turn_queries_and_keys(following[0], following[1])
-            if c == 0 and b + 1 < B:
-                if h == 0:
-                    raw_of[b + 1] = load_batch(b + 1)
-                if h == 1:
-                    values_of[b + 1] = project_values(raw_of[b + 1][1])
-                if h == 2:
-                    maskT_of[b + 1] = turn_mask(raw_of[b + 1][0])
-            if n + AHEAD < len(chunks):
-                later = chunks[n + AHEAD]
-                term_of[later] = build_term(later[0], later[1], later[2], maskT_of[later[0]])
-            qT, kT = turned_of[(b, h)]
-            v_codes, v_scales = values_of[b]
-            attend(b, h, c, qT, kT, term_of[(b, h, c)], v_codes, v_scales)
+        for k in range(ALL_ROWS + 6):
+            if k < ALL_ROWS:
+                if k % ROWS == 0 and k // ROWS + AHEAD < ALL_CHUNKS:
+                    build_term(k // ROWS + AHEAD)
+                fill_scores(k, 0)
+            if 0 <= k - 3 < ALL_ROWS:
+                quantise_e(k - 3)
+            if k >= 5 and (k - 5) % ROWS == ROWS - 1:
+                finish((k - 5) // ROWS)
+            if 0 <= k - 2 < ALL_ROWS:
+                turn_e(k - 2)
+            if k < ALL_ROWS:
+                fill_scores(k, 1)
+                find_shift(k)
+            if 0 <= k - 1 < ALL_ROWS:
+                exponentials(k - 1)
+            if 0 <= k - 2 < ALL_ROWS:
+                group_e(k - 2)
+            if k < ALL_ROWS:
+                prepare(k // TILES, k % TILES)
+            if 4 <= k < ALL_ROWS + 4 and (k - 4) % ROWS == ROWS - 1:
+                weigh_values((k - 4) // ROWS)

@@ -280,7 +280,8 @@ def tile_fastbloomattention_pa_t_kernel(
 
         def group_e(k):
             e_grouped[k] = per_row.tile([P, S], BF16, align_bytes=64, name="e_grp")
-            interleave_out_of_psum(nc.scalar.copy, e_grouped[k], eT[k])
+            copy = nc.scalar.copy if k % 2 == 0 else nc.vector.tensor_copy
+            interleave_out_of_psum(copy, e_grouped[k], eT[k])
 
         def quantise_e(k):
             n, r = k // ROWS, k % ROWS

@@ -30,10 +30,9 @@ SQRT_D = math.sqrt(D)
 FLOPS = 2 * B * S * HD * HD + 2 * 2 * B * H * S * S * D
 
 
-def interleave_out_of_psum(copy, grouped, planes):
-    copy(
-        out=grouped[:].rearrange("p (c u w) -> p c u w", u=2, w=2),
-        in_=planes[:].bitcast(BF16).rearrange("p (u c w) -> p c u w", u=2, w=2),
+def turn_words(nc, bank, column, u, words, identity):
+    nc.tensor.transpose(
+        bank[:].rearrange("p (c u) -> p c u", u=2)[:, column : column + P, u], words, identity
     )
 
 
@@ -145,14 +144,11 @@ def tile_fastbloomattention_pa_t_kernel(
             hid_ps = psum_turn.tile([P, BANK], F32, tag="turn")
             for u in range(2):
                 for w in range(2):
-                    spot = (u * 2 + w) * P
-                    nc.tensor.transpose(
-                        hid_ps[:, spot : spot + P],
-                        hid_words[:, j, w, u * P : (u + 1) * P],
-                        ident_f32[:],
+                    turn_words(
+                        nc, hid_ps, w * P, u, hid_words[:, j, w, u * P : (u + 1) * P], ident_f32[:]
                     )
             h_grp = stage.tile([P, 2 * P * 4], BF16, align_bytes=64)
-            interleave_out_of_psum(nc.vector.tensor_copy, h_grp, hid_ps)
+            nc.vector.tensor_copy(out=h_grp[:], in_=hid_ps[:].bitcast(BF16))
             block = slice(j * 2 * P, (j + 1) * 2 * P)
             nc.vector.quantize_mx(
                 out=h_codes[:, block].bitcast(FP8X4), scales=h_scales[:, block], in_=h_grp[:]
@@ -272,16 +268,14 @@ def tile_fastbloomattention_pa_t_kernel(
             eT[k] = psum_turn.tile([P, BANK], F32, tag="turn", name="eT_ps")
             for g in range(PASSES):
                 for u in range(2):
-                    nc.tensor.transpose(
-                        eT[k][:, (u * PASSES + g) * P : (u * PASSES + g + 1) * P],
-                        e_words[:, (2 * g + u) * P : (2 * g + u + 1) * P],
+                    turn_words(
+                        nc, eT[k], g * P, u, e_words[:, (2 * g + u) * P : (2 * g + u + 1) * P],
                         ident_f32[:],
                     )
 
         def group_e(k):
             e_grouped[k] = per_row.tile([P, S], BF16, align_bytes=64, name="e_grp")
-            copy = nc.scalar.copy if k % 2 == 0 else nc.vector.tensor_copy
-            interleave_out_of_psum(copy, e_grouped[k], eT[k])
+            nc.scalar.copy(out=e_grouped[k][:], in_=eT[k][:].bitcast(BF16))
 
         def quantise_e(k):
             n, r = k // ROWS, k % ROWS

@@ -203,39 +203,45 @@ def tile_fastbloomattention_pa_t_kernel(
                 turn_mask(b + 1, 4 * h + i - 2)
             if h == 1 and i == 6 and b + 2 < B:
                 load_mask(b + 2)
-            if h >= 2 and i < 4:
-                quantise_hidden(b + 1, 2 * (h - 2) + i - 2)
-            if h >= 2 and i >= 4:
-                project_values(b + 1, h - 2, i - 4)
             if h == 3 and i == 7 and b + 2 < B:
                 load_hidden(b + 2)
 
-        def fill_scores(k, half):
-            n, r = k // ROWS, k % ROWS
+        def prepare_values(n, i):
+            b, h = n // H, n % H
+            if b + 1 < B and h >= 2 and 2 <= i < 4:
+                quantise_hidden(b + 1, 2 * (h - 2) + i - 2)
+            if b + 1 < B and h >= 2 and i >= 4:
+                project_values(b + 1, h - 2, i - 4)
+
+        def multiply_keys(k):
             queries = slice((k % TILES) * P, (k % TILES + 1) * P)
-            if half == 0:
-                tops[k] = per_row.tile([P, 2], F32, name="tops")
-            bank = psum_scores.tile([P, BANK], F32, tag="scores")
-            nc.tensor.matmul(
-                bank[:],
-                lhsT=qk_turned[("q", k // TILES)][:, queries],
-                rhs=qk_turned[("k", k // TILES)][:, half * BANK : (half + 1) * BANK],
-                start=True,
-                stop=False,
-            )
-            for a in range(4):
+            for half in range(2):
+                scores[(k, half)] = psum_scores.tile([P, BANK], F32, tag="scores", name="bank")
                 nc.tensor.matmul(
-                    bank[:, a * P : (a + 1) * P],
-                    lhsT=term[n][:, 4 * half + a, r * P : (r + 1) * P],
-                    rhs=ident_f32[:],
-                    start=False,
-                    stop=(a == 3),
-                    is_transpose=True,
+                    scores[(k, half)][:],
+                    lhsT=qk_turned[("q", k // TILES)][:, queries],
+                    rhs=qk_turned[("k", k // TILES)][:, half * BANK : (half + 1) * BANK],
+                    start=True,
+                    stop=False,
                 )
-            nc.vector.tensor_reduce(
-                out=tops[k][:, half : half + 1], in_=bank[:], axis=AXIS.X, op=ALU.max
-            )
-            scores[(k, half)] = bank
+
+        def add_term(k):
+            n, r = k // ROWS, k % ROWS
+            tops[k] = per_row.tile([P, 2], F32, name="tops")
+            for half in range(2):
+                bank = scores[(k, half)]
+                for a in range(4):
+                    nc.tensor.matmul(
+                        bank[:, a * P : (a + 1) * P],
+                        lhsT=term[n][:, 4 * half + a, r * P : (r + 1) * P],
+                        rhs=ident_f32[:],
+                        start=False,
+                        stop=(a == 3),
+                        is_transpose=True,
+                    )
+                nc.vector.tensor_reduce(
+                    out=tops[k][:, half : half + 1], in_=bank[:], axis=AXIS.X, op=ALU.max
+                )
 
         def find_shift(k):
             shift[k] = per_row.tile([P, 1], F32, name="shift")
@@ -380,21 +386,23 @@ def tile_fastbloomattention_pa_t_kernel(
             if k < ALL_ROWS:
                 if k % ROWS == 0 and k // ROWS + AHEAD < ALL_CHUNKS:
                     build_term(k // ROWS + AHEAD)
-                fill_scores(k, 0)
+                multiply_keys(k)
             if 0 <= k - 3 < ALL_ROWS:
                 quantise_e(k - 3)
             if k >= 5 and (k - 5) % ROWS == ROWS - 1:
                 finish((k - 5) // ROWS)
+            if k < ALL_ROWS:
+                add_term(k)
+                find_shift(k)
             if 0 <= k - 2 < ALL_ROWS:
                 turn_e(k - 2)
-            if k < ALL_ROWS:
-                fill_scores(k, 1)
-                find_shift(k)
             if 0 <= k - 1 < ALL_ROWS:
                 exponentials(k - 1)
             if 0 <= k - 2 < ALL_ROWS:
                 group_e(k - 2)
             if k < ALL_ROWS:
-                prepare(k // TILES, k % TILES)
+                prepare_values(k // TILES, k % TILES)
             if 4 <= k < ALL_ROWS + 4 and (k - 4) % ROWS == ROWS - 1:
                 weigh_values((k - 4) // ROWS)
+            if k < ALL_ROWS:
+                prepare(k // TILES, k % TILES)

@@ -64,6 +64,7 @@ def tile_fastbloomattention_pa_t_kernel(
         h_quantised, v_grouped, v_quantised = {}, {}, {}
         term, scores, tops, shift, e, eT, e_grouped = {}, {}, {}, {}, {}, {}, {}
         e_quantised, part_sums, context_ps = {}, {}, {}
+        sums, inverse = {}, {}
 
         def load_queries_and_keys(n):
             for label, source in (("q", query), ("k", key)):
@@ -225,23 +226,23 @@ def tile_fastbloomattention_pa_t_kernel(
                     stop=False,
                 )
 
-        def add_term(k):
+        def add_term(k, half):
             n, r = k // ROWS, k % ROWS
-            tops[k] = per_row.tile([P, 2], F32, name="tops")
-            for half in range(2):
-                bank = scores[(k, half)]
-                for a in range(4):
-                    nc.tensor.matmul(
-                        bank[:, a * P : (a + 1) * P],
-                        lhsT=term[n][:, 4 * half + a, r * P : (r + 1) * P],
-                        rhs=ident_f32[:],
-                        start=False,
-                        stop=(a == 3),
-                        is_transpose=True,
-                    )
-                nc.vector.tensor_reduce(
-                    out=tops[k][:, half : half + 1], in_=bank[:], axis=AXIS.X, op=ALU.max
+            if half == 0:
+                tops[k] = per_row.tile([P, 2], F32, name="tops")
+            bank = scores[(k, half)]
+            for a in range(4):
+                nc.tensor.matmul(
+                    bank[:, a * P : (a + 1) * P],
+                    lhsT=term[n][:, 4 * half + a, r * P : (r + 1) * P],
+                    rhs=ident_f32[:],
+                    start=False,
+                    stop=(a == 3),
+                    is_transpose=True,
                 )
+            nc.vector.tensor_reduce(
+                out=tops[k][:, half : half + 1], in_=bank[:], axis=AXIS.X, op=ALU.max
+            )
 
         def find_shift(k):
             shift[k] = per_row.tile([P, 1], F32, name="shift")
@@ -317,17 +318,21 @@ def tile_fastbloomattention_pa_t_kernel(
                         stop=(g == PASSES - 1),
                     )
 
+        def sum_rows(n):
+            sums[n] = per_chunk.tile([P, ROWS], F32, name="sums")
+            nc.vector.tensor_reduce(out=sums[n][:], in_=part_sums[n][:], axis=AXIS.X, op=ALU.add)
+
+        def invert_sums(n):
+            inverse[n] = per_chunk.tile([P, ROWS], F32, name="inverse")
+            nc.vector.reciprocal(out=inverse[n][:], in_=sums[n][:])
+
         def finish(n):
             b, h, c = n // (H * CHUNKS), (n // CHUNKS) % H, n % CHUNKS
-            sums = per_chunk.tile([P, ROWS], F32)
-            nc.vector.tensor_reduce(out=sums[:], in_=part_sums[n][:], axis=AXIS.X, op=ALU.add)
-            inverse = per_chunk.tile([P, ROWS], F32)
-            nc.vector.reciprocal(out=inverse[:], in_=sums[:])
             context = per_chunk.tile([P, ROWS, D], F32)
             nc.vector.tensor_tensor(
                 out=context[:],
                 in0=context_ps[n][:].rearrange("p (r d) -> p r d", r=ROWS),
-                in1=inverse[:].unsqueeze(2).to_broadcast([P, ROWS, D]),
+                in1=inverse[n][:].unsqueeze(2).to_broadcast([P, ROWS, D]),
                 op=ALU.mult,
             )
             nc.sync.dma_start(
@@ -387,13 +392,21 @@ def tile_fastbloomattention_pa_t_kernel(
                 if k % ROWS == 0 and k // ROWS + AHEAD < ALL_CHUNKS:
                     build_term(k // ROWS + AHEAD)
                 multiply_keys(k)
+            chunk_done = k >= 5 and (k - 5) % ROWS == ROWS - 1
+            if chunk_done:
+                sum_rows((k - 5) // ROWS)
+            if k < ALL_ROWS:
+                add_term(k, 0)
+            if chunk_done:
+                invert_sums((k - 5) // ROWS)
+            if k < ALL_ROWS:
+                add_term(k, 1)
             if 0 <= k - 3 < ALL_ROWS:
                 quantise_e(k - 3)
-            if k >= 5 and (k - 5) % ROWS == ROWS - 1:
-                finish((k - 5) // ROWS)
             if k < ALL_ROWS:
-                add_term(k)
                 find_shift(k)
+            if chunk_done:
+                finish((k - 5) // ROWS)
             if 0 <= k - 2 < ALL_ROWS:
                 turn_e(k - 2)
             if 0 <= k - 1 < ALL_ROWS:

@@ -84,19 +84,19 @@ def tile_fastbloomattention_pa_t_kernel(
             nc.scalar.copy(out=kept[:], in_=turned_ps[:])
             qk_turned[(label, n)] = kept
 
-        def load_mask(b):
-            loaded = raw.tile([P, TILES, S], BF16, name="mask_raw")
-            mask_rows = attention_mask[b, 0].rearrange("(t p) k -> p t k", p=P)
-            for c in range(CHUNKS):
-                its = slice(c * ROWS, (c + 1) * ROWS)
-                nc.sync.dma_start(out=loaded[:, its, :], in_=mask_rows[:, its, :])
-            mask_raw[b] = loaded
+        def load_mask(b, c):
+            if c == 0:
+                mask_raw[b] = raw.tile([P, TILES, S], BF16, name="mask_raw")
+            its = slice(c * ROWS, (c + 1) * ROWS)
+            nc.sync.dma_start(
+                out=mask_raw[b][:, its, :],
+                in_=attention_mask[b, 0].rearrange("(t p) k -> p t k", p=P)[:, its, :],
+            )
 
-        def turn_mask(b, piece):
+        def turn_mask_in_psum(b, piece, mask_ps):
             c, pair = piece // 4, piece % 4
             if piece == 0:
                 maskT[b] = per_batch.tile([P, TILES, S], BF16, name="maskT")
-            mask_ps = psum_turn.tile([P, 2 * BANK], BF16, tag="turn")
             for a in range(2):
                 kt = 2 * pair + a
                 for r in range(ROWS):
@@ -106,10 +106,46 @@ def tile_fastbloomattention_pa_t_kernel(
                         mask_raw[b][:, c * ROWS + r, kt * P : (kt + 1) * P],
                         ident_bf[:],
                     )
-            nc.vector.tensor_copy(
+
+        def keep_mask(b, piece, mask_ps, copy):
+            c, pair = piece // 4, piece % 4
+            copy(
                 out=maskT[b][:, 2 * pair : 2 * pair + 2, c * BANK : (c + 1) * BANK],
                 in_=mask_ps[:].rearrange("p (a i) -> p a i", a=2),
             )
+
+        def turn_mask(b, piece):
+            mask_ps = psum_turn.tile([P, 2 * BANK], BF16, tag="turn")
+            turn_mask_in_psum(b, piece, mask_ps)
+            keep_mask(b, piece, mask_ps, nc.vector.tensor_copy)
+
+        def build_first_term():
+            built = terms.tile([P, TILES, BANK], F32, name="term")
+            for piece in range(4):
+                mask_ps = psum_scores.tile([P, 2 * BANK], BF16, tag="scores")
+                turn_mask_in_psum(0, piece, mask_ps)
+                for a in range(2):
+                    kt = 2 * piece + a
+                    turned = mask_ps[:, a * BANK : (a + 1) * BANK]
+                    if piece % 2 == 0:
+                        nc.vector.tensor_scalar(
+                            out=built[:, kt, :],
+                            in0=turned,
+                            scalar1=SQRT_D,
+                            scalar2=alibi_cols[:, kt : kt + 1],
+                            op0=ALU.mult,
+                            op1=ALU.add,
+                        )
+                    else:
+                        nc.scalar.activation(
+                            out=built[:, kt, :],
+                            in_=turned,
+                            func=ACT.Identity,
+                            bias=alibi_cols[:, kt : kt + 1],
+                            scale=SQRT_D,
+                        )
+                keep_mask(0, piece, mask_ps, nc.vector.tensor_copy if piece % 2 == 0 else nc.scalar.copy)
+            term[0] = built
 
         def build_term(n):
             head, c = n // CHUNKS, n % CHUNKS
@@ -155,7 +191,7 @@ def tile_fastbloomattention_pa_t_kernel(
                 out=h_codes[:, block].bitcast(FP8X4), scales=h_scales[:, block], in_=h_grp[:]
             )
 
-        def project_values(b, g, h):
+        def project_values(b, g, h, pool=psum_mx, tag="mx"):
             if (g, h) == (0, 0):
                 v_quantised[b] = (
                     per_batch.tile([P, PASSES * HD], U32, align_bytes=64, name="v_codes"),
@@ -165,7 +201,7 @@ def tile_fastbloomattention_pa_t_kernel(
                 v_grouped[b] = stage.tile([P, HD * 4], BF16, align_bytes=64, name="v_grp")
             h_codes, h_scales = h_quantised[b]
             head = slice(h * D, (h + 1) * D)
-            v_ps = psum_mx.tile([P, BANK], F32, tag="mx")
+            v_ps = pool.tile([P, BANK], F32, tag=tag, name="v_ps")
             for t in range(4):
                 keys = slice((4 * g + t) * P, (4 * g + t + 1) * P)
                 nc.tensor.matmul_mx(
@@ -198,12 +234,13 @@ def tile_fastbloomattention_pa_t_kernel(
                 turn_queries_or_keys("qk"[i], n + 1)
             if i == 2 and n + 2 < B * H:
                 load_queries_and_keys(n + 2)
-            if i < 2 or b + 1 >= B:
+            if b + 1 >= B:
                 return
-            if h < 2 and i < 6:
-                turn_mask(b + 1, 4 * h + i - 2)
-            if h == 1 and i == 6 and b + 2 < B:
-                load_mask(b + 2)
+            if h < 2 and i >= 4:
+                turn_mask(b + 1, 4 * h + i - 4)
+            if h == 2 and i == 0 and b + 2 < B:
+                load_mask(b + 2, 0)
+                load_mask(b + 2, 1)
             if h == 3 and i == 7 and b + 2 < B:
                 load_hidden(b + 2)
 
@@ -347,16 +384,17 @@ def tile_fastbloomattention_pa_t_kernel(
             out=alibi_rows[:], in_=alibi.rearrange("b h o (t k) -> (b h o t) k", k=P)
         )
         load_queries_and_keys(0)
-        load_mask(0)
+        load_mask(0, 0)
         w_raw = const.tile([P, 4, HD], BF16)
         nc.sync.dma_start(
             out=w_raw[:].rearrange("p (u w) x -> p u (w x)", u=2),
             in_=W_value.rearrange("(u p w) x -> p u (w x)", u=2, w=2),
         )
+        load_mask(0, 1)
+        load_queries_and_keys(1)
+        load_hidden(0)
         bias_bc = const.tile([P, HD], BF16)
         nc.sync.dma_start(out=bias_bc[:], in_=b_value.partition_broadcast(P))
-        load_hidden(0)
-        load_queries_and_keys(1)
 
         alibi_ps = psum_turn.tile([P, P], BF16, tag="turn")
         nc.tensor.transpose(alibi_ps[:], alibi_rows[:], ident_bf[:])
@@ -366,47 +404,64 @@ def tile_fastbloomattention_pa_t_kernel(
         )
         turn_queries_or_keys("q", 0)
         turn_queries_or_keys("k", 0)
-        for c in range(CHUNKS):
-            for pair in range(4):
-                turn_mask(0, 4 * c + pair)
-            build_term(c)
-        load_mask(1)
+        build_first_term()
         w_grp = const.tile([P, HD, 4], BF16, align_bytes=64)
-        nc.vector.tensor_copy(out=w_grp[:], in_=w_raw[:].rearrange("p t x -> p x t"))
         w_codes = const.tile([P, HD], U32, align_bytes=64)
         w_scales = const.tile([P, HD], U8, align_bytes=64)
-        nc.vector.quantize_mx(
-            out=w_codes[:].bitcast(FP8X4),
-            scales=w_scales[:],
-            in_=w_grp[:].rearrange("p x t -> p (x t)"),
-        )
-        for j in range(4):
-            quantise_hidden(0, j)
-        load_hidden(1)
-        for g in range(PASSES):
-            for h in range(H):
+
+        def prepare_first_batch(k):
+            if k == 0:
+                turn_mask(0, 4)
+                turn_mask(0, 5)
+                nc.scalar.copy(out=w_grp[:], in_=w_raw[:].rearrange("p t x -> p x t"))
+            if k == 1:
+                turn_mask(0, 6)
+                turn_mask(0, 7)
+                build_term(1)
+                load_mask(1, 0)
+                load_mask(1, 1)
+                nc.vector.quantize_mx(
+                    out=w_codes[:].bitcast(FP8X4),
+                    scales=w_scales[:],
+                    in_=w_grp[:].rearrange("p x t -> p (x t)"),
+                )
+            if k == 2 or k == 3:
+                quantise_hidden(0, 2 * (k - 2))
+                quantise_hidden(0, 2 * (k - 2) + 1)
+            if k == 3:
+                load_hidden(1)
+            if 4 <= k < 8:
+                g, h = (k - 4) // 2, 2 * ((k - 4) % 2)
                 project_values(0, g, h)
+                project_values(0, g, h + 1, psum_turn, "turn")
+
+        def weighed_in(k):
+            if k == 8:
+                return 0
+            if k > 8 and k % ROWS == ROWS - 1 and k - 7 < ALL_ROWS:
+                return (k - 7) // ROWS
+            return None
 
         for k in range(ALL_ROWS + 6):
             if k < ALL_ROWS:
-                if k % ROWS == 0 and k // ROWS + AHEAD < ALL_CHUNKS:
+                if k > 0 and k % ROWS == 0 and k // ROWS + AHEAD < ALL_CHUNKS:
                     build_term(k // ROWS + AHEAD)
                 multiply_keys(k)
-            chunk_done = k >= 5 and (k - 5) % ROWS == ROWS - 1
-            if chunk_done:
-                sum_rows((k - 5) // ROWS)
+            done = weighed_in(k - 1)
+            if done is not None:
+                sum_rows(done)
             if k < ALL_ROWS:
                 add_term(k, 0)
-            if chunk_done:
-                invert_sums((k - 5) // ROWS)
+            if done is not None:
+                invert_sums(done)
             if k < ALL_ROWS:
                 add_term(k, 1)
             if 0 <= k - 3 < ALL_ROWS:
                 quantise_e(k - 3)
             if k < ALL_ROWS:
                 find_shift(k)
-            if chunk_done:
-                finish((k - 5) // ROWS)
+            if done is not None:
+                finish(done)
             if 0 <= k - 2 < ALL_ROWS:
                 turn_e(k - 2)
             if 0 <= k - 1 < ALL_ROWS:
@@ -415,7 +470,10 @@ def tile_fastbloomattention_pa_t_kernel(
                 group_e(k - 2)
             if k < ALL_ROWS:
                 prepare_values(k // TILES, k % TILES)
-            if 4 <= k < ALL_ROWS + 4 and (k - 4) % ROWS == ROWS - 1:
-                weigh_values((k - 4) // ROWS)
+            if weighed_in(k) is not None:
+                weigh_values(weighed_in(k))
             if k < ALL_ROWS:
+                prepare_first_batch(k)
                 prepare(k // TILES, k % TILES)
+            if k == 2:
+                build_term(2)

@@ -45,13 +45,12 @@ def tile_fastbloomattention_pa_t_kernel(
         raw = pools.enter_context(tc.tile_pool(name="raw", bufs=1))
         per_batch = pools.enter_context(tc.tile_pool(name="per_batch", bufs=2))
         per_head = pools.enter_context(tc.tile_pool(name="per_head", bufs=2))
-        terms = pools.enter_context(tc.tile_pool(name="terms", bufs=AHEAD + 1))
+        terms = pools.enter_context(tc.tile_pool(name="terms", bufs=AHEAD + 2))
         stage = pools.enter_context(tc.tile_pool(name="stage", bufs=2))
         per_row = pools.enter_context(tc.tile_pool(name="per_row", bufs=3))
         per_chunk = pools.enter_context(tc.tile_pool(name="per_chunk", bufs=3))
         psum_scores = pools.enter_context(tc.psum_pool(name="psum_scores", bufs=4))
-        psum_turn = pools.enter_context(tc.psum_pool(name="psum_turn", bufs=3))
-        psum_mx = pools.enter_context(tc.psum_pool(name="psum_mx", bufs=1))
+        psum_turn = pools.enter_context(tc.psum_pool(name="psum_turn", bufs=4))
 
         ident_bf = const.tile([P, P], BF16)
         make_identity(nc, ident_bf[:])
@@ -191,7 +190,7 @@ def tile_fastbloomattention_pa_t_kernel(
                 out=h_codes[:, block].bitcast(FP8X4), scales=h_scales[:, block], in_=h_grp[:]
             )
 
-        def project_values(b, g, h, pool=psum_mx, tag="mx"):
+        def project_values(b, g, h):
             if (g, h) == (0, 0):
                 v_quantised[b] = (
                     per_batch.tile([P, PASSES * HD], U32, align_bytes=64, name="v_codes"),
@@ -201,7 +200,7 @@ def tile_fastbloomattention_pa_t_kernel(
                 v_grouped[b] = stage.tile([P, HD * 4], BF16, align_bytes=64, name="v_grp")
             h_codes, h_scales = h_quantised[b]
             head = slice(h * D, (h + 1) * D)
-            v_ps = pool.tile([P, BANK], F32, tag=tag, name="v_ps")
+            v_ps = psum_turn.tile([P, BANK], F32, tag="turn", name="v_ps")
             for t in range(4):
                 keys = slice((4 * g + t) * P, (4 * g + t + 1) * P)
                 nc.tensor.matmul_mx(
@@ -340,7 +339,7 @@ def tile_fastbloomattention_pa_t_kernel(
             b, h = n // (H * CHUNKS), (n // CHUNKS) % H
             e_codes, e_scales = e_quantised[n]
             v_codes, v_scales = v_quantised[b]
-            context_ps[n] = psum_mx.tile([P, BANK], F32, tag="mx", name="context_ps")
+            context_ps[n] = psum_turn.tile([P, BANK], F32, tag="turn", name="context_ps")
             for r in range(ROWS):
                 for g in range(PASSES):
                     mine = slice((r * PASSES + g) * P, (r * PASSES + g + 1) * P)
@@ -433,7 +432,7 @@ def tile_fastbloomattention_pa_t_kernel(
             if 4 <= k < 8:
                 g, h = (k - 4) // 2, 2 * ((k - 4) % 2)
                 project_values(0, g, h)
-                project_values(0, g, h + 1, psum_turn, "turn")
+                project_values(0, g, h + 1)
 
         def weighed_in(k):
             if k == 8:
@@ -456,12 +455,12 @@ def tile_fastbloomattention_pa_t_kernel(
                 invert_sums(done)
             if k < ALL_ROWS:
                 add_term(k, 1)
+            if done is not None:
+                finish(done)
             if 0 <= k - 3 < ALL_ROWS:
                 quantise_e(k - 3)
             if k < ALL_ROWS:
                 find_shift(k)
-            if done is not None:
-                finish(done)
             if 0 <= k - 2 < ALL_ROWS:
                 turn_e(k - 2)
             if 0 <= k - 1 < ALL_ROWS:

@@ -66,12 +66,14 @@ def tile_fastbloomattention_pa_t_kernel(
         sums, inverse = {}, {}
 
         def load_queries_and_keys(n):
-            for label, source in (("q", query), ("k", key)):
-                loaded = per_head.tile([P, TILES, D], BF16, name=label + "_raw")
-                nc.sync.dma_start(
-                    out=loaded[:], in_=source[n // H, n % H].rearrange("(t p) d -> p t d", p=P)
-                )
-                qk_raw[(label, n)] = loaded
+            q_raw = per_head.tile([P, TILES, D], BF16)
+            nc.sync.dma_start(out=q_raw[:], in_=query[n // H, n % H].rearrange("(t p) d -> p t d", p=P))
+            k_raw = per_head.tile([P, TILES, D], BF16)
+            nc.sync.dma_start(
+                out=k_raw[:].rearrange("p (j w) d -> p j (w d)", w=2),
+                in_=key[n // H, n % H].rearrange("(j p w) d -> p j (w d)", p=P, w=2),
+            )
+            qk_raw[("q", n)], qk_raw[("k", n)] = q_raw, k_raw
 
         def turn_queries_or_keys(label, n):
             turned_ps = psum_turn.tile([P, S], BF16, tag="turn", name=label + "_ps")
@@ -93,39 +95,38 @@ def tile_fastbloomattention_pa_t_kernel(
             )
 
         def turn_mask_in_psum(b, piece, mask_ps):
-            c, pair = piece // 4, piece % 4
+            c, j = piece // 4, piece % 4
             if piece == 0:
-                maskT[b] = per_batch.tile([P, TILES, S], BF16, name="maskT")
-            for a in range(2):
-                kt = 2 * pair + a
-                for r in range(ROWS):
-                    spot = (a * ROWS + r) * P
-                    nc.tensor.transpose(
-                        mask_ps[:, spot : spot + P],
-                        mask_raw[b][:, c * ROWS + r, kt * P : (kt + 1) * P],
-                        ident_bf[:],
-                    )
+                maskT[b] = per_batch.tile([P, 4, S, 2], BF16, name="maskT")
+            words = mask_raw[b][:].rearrange("p t k -> p (t k)").bitcast(F32)
+            words = words.rearrange("p (t x) -> p t x", t=TILES)
+            for r in range(ROWS):
+                nc.tensor.transpose(
+                    mask_ps[:, r * P : (r + 1) * P],
+                    words[:, c * ROWS + r, j * P : (j + 1) * P],
+                    ident_f32[:],
+                )
 
         def keep_mask(b, piece, mask_ps, copy):
-            c, pair = piece // 4, piece % 4
+            c, j = piece // 4, piece % 4
             copy(
-                out=maskT[b][:, 2 * pair : 2 * pair + 2, c * BANK : (c + 1) * BANK],
-                in_=mask_ps[:].rearrange("p (a i) -> p a i", a=2),
+                out=maskT[b][:, j, c * BANK : (c + 1) * BANK, :].rearrange("p i w -> p (i w)"),
+                in_=mask_ps[:].bitcast(BF16),
             )
 
         def turn_mask(b, piece):
-            mask_ps = psum_turn.tile([P, 2 * BANK], BF16, tag="turn")
+            mask_ps = psum_turn.tile([P, BANK], F32, tag="turn")
             turn_mask_in_psum(b, piece, mask_ps)
             keep_mask(b, piece, mask_ps, nc.vector.tensor_copy)
 
         def build_first_term():
             built = terms.tile([P, TILES, BANK], F32, name="term")
             for piece in range(4):
-                mask_ps = psum_scores.tile([P, 2 * BANK], BF16, tag="scores")
+                mask_ps = psum_scores.tile([P, BANK], F32, tag="scores")
                 turn_mask_in_psum(0, piece, mask_ps)
-                for a in range(2):
-                    kt = 2 * piece + a
-                    turned = mask_ps[:, a * BANK : (a + 1) * BANK]
+                for w in range(2):
+                    kt = 2 * piece + w
+                    turned = mask_ps[:].bitcast(BF16).rearrange("p (i w) -> p i w", w=2)[:, :, w]
                     if piece % 2 == 0:
                         nc.vector.tensor_scalar(
                             out=built[:, kt, :],
@@ -153,7 +154,7 @@ def tile_fastbloomattention_pa_t_kernel(
                 column = head * TILES + kt
                 nc.gpsimd.tensor_scalar(
                     out=built[:, kt, :],
-                    in0=maskT[head // H][:, kt, c * BANK : (c + 1) * BANK],
+                    in0=maskT[head // H][:, kt // 2, c * BANK : (c + 1) * BANK, kt % 2],
                     scalar1=SQRT_D,
                     scalar2=alibi_cols[:, column : column + 1],
                     op0=ALU.mult,
@@ -163,10 +164,14 @@ def tile_fastbloomattention_pa_t_kernel(
 
         def load_hidden(b):
             loaded = raw.tile([P, 4 * 2 * HD], BF16, name="hid_raw")
-            nc.sync.dma_start(
-                out=loaded[:].rearrange("p (j c) -> p j c", j=4),
-                in_=hidden_states[b].rearrange("(j p w) c -> p j (w c)", j=4, w=2),
-            )
+            for a in range(2):
+                for s in range(2):
+                    nc.sync.dma_start(
+                        out=loaded[a * P // 2 : (a + 1) * P // 2, :].rearrange(
+                            "y (j s c) -> y j s c", j=4, s=2
+                        )[:, :, s, :],
+                        in_=hidden_states[b].rearrange("(j y s a) c -> a s y j c", j=4, s=2, a=2)[a, s],
+                    )
             hid_raw[b] = loaded
 
         def quantise_hidden(b, j):
@@ -176,12 +181,12 @@ def tile_fastbloomattention_pa_t_kernel(
                     stage.tile([P, 4 * 2 * P], U8, align_bytes=64, name="h_scales"),
                 )
             h_codes, h_scales = h_quantised[b]
-            hid_words = hid_raw[b][:].bitcast(F32).rearrange("p (j w x) -> p j w x", j=4, w=2)
+            hid_words = hid_raw[b][:].bitcast(F32).rearrange("p (j s x) -> p j s x", j=4, s=2)
             hid_ps = psum_turn.tile([P, BANK], F32, tag="turn")
             for u in range(2):
-                for w in range(2):
+                for s in range(2):
                     turn_words(
-                        nc, hid_ps, w * P, u, hid_words[:, j, w, u * P : (u + 1) * P], ident_f32[:]
+                        nc, hid_ps, s * P, u, hid_words[:, j, s, u * P : (u + 1) * P], ident_f32[:]
                     )
             h_grp = stage.tile([P, 2 * P * 4], BF16, align_bytes=64)
             nc.vector.tensor_copy(out=h_grp[:], in_=hid_ps[:].bitcast(BF16))
@@ -235,8 +240,6 @@ def tile_fastbloomattention_pa_t_kernel(
                 load_queries_and_keys(n + 2)
             if b + 1 >= B:
                 return
-            if h < 2 and i >= 4:
-                turn_mask(b + 1, 4 * h + i - 4)
             if h == 2 and i == 0 and b + 2 < B:
                 load_mask(b + 2, 0)
                 load_mask(b + 2, 1)
@@ -245,6 +248,8 @@ def tile_fastbloomattention_pa_t_kernel(
 
         def prepare_values(n, i):
             b, h = n // H, n % H
+            if b + 1 < B and h < 2 and i >= 4:
+                turn_mask(b + 1, 4 * h + i - 4)
             if b + 1 < B and h >= 2 and 2 <= i < 4:
                 quantise_hidden(b + 1, 2 * (h - 2) + i - 2)
             if b + 1 < B and h >= 2 and i >= 4:
@@ -317,8 +322,9 @@ def tile_fastbloomattention_pa_t_kernel(
                     )
 
         def group_e(k):
-            e_grouped[k] = per_row.tile([P, S], BF16, align_bytes=64, name="e_grp")
-            nc.scalar.copy(out=e_grouped[k][:], in_=eT[k][:].bitcast(BF16))
+            if k % 2 == 0:
+                e_grouped[k // 2] = per_row.tile([P, 2, S], BF16, align_bytes=64, name="e_grp")
+            nc.scalar.copy(out=e_grouped[k // 2][:, k % 2, :], in_=eT[k][:].bitcast(BF16))
 
         def quantise_e(k):
             n, r = k // ROWS, k % ROWS
@@ -328,11 +334,11 @@ def tile_fastbloomattention_pa_t_kernel(
                     per_chunk.tile([P, ROWS * PASSES * P], U8, align_bytes=64, name="e_scales"),
                 )
             e_codes, e_scales = e_quantised[n]
-            mine = slice(r * PASSES * P, (r + 1) * PASSES * P)
+            ours = slice(r * PASSES * P, (r + 2) * PASSES * P)
             nc.vector.quantize_mx(
-                out=e_codes[:, mine].bitcast(FP8X4),
-                scales=e_scales[:, mine],
-                in_=e_grouped[k][:],
+                out=e_codes[:, ours].bitcast(FP8X4),
+                scales=e_scales[:, ours],
+                in_=e_grouped[k // 2][:].rearrange("p a s -> p (a s)"),
             )
 
         def weigh_values(n):
@@ -378,10 +384,12 @@ def tile_fastbloomattention_pa_t_kernel(
                 in_=context[:],
             )
 
-        alibi_rows = const.tile([P, P], BF16)
-        nc.sync.dma_start(
-            out=alibi_rows[:], in_=alibi.rearrange("b h o (t k) -> (b h o t) k", k=P)
-        )
+        alibi_rows = const.tile([P, 2 * P], BF16)
+        for half in range(2):
+            nc.sync.dma_start(
+                out=alibi_rows[half * P // 2 : (half + 1) * P // 2, :],
+                in_=alibi.rearrange("b h o (j k) -> (b h o j) k", k=2 * P),
+            )
         load_queries_and_keys(0)
         load_mask(0, 0)
         w_raw = const.tile([P, 4, HD], BF16)
@@ -395,11 +403,11 @@ def tile_fastbloomattention_pa_t_kernel(
         bias_bc = const.tile([P, HD], BF16)
         nc.sync.dma_start(out=bias_bc[:], in_=b_value.partition_broadcast(P))
 
-        alibi_ps = psum_turn.tile([P, P], BF16, tag="turn")
-        nc.tensor.transpose(alibi_ps[:], alibi_rows[:], ident_bf[:])
+        alibi_ps = psum_turn.tile([P, P], F32, tag="turn")
+        nc.tensor.transpose(alibi_ps[:], alibi_rows[:].bitcast(F32), ident_f32[:])
         alibi_cols = const.tile([P, P], F32)
         nc.vector.tensor_scalar(
-            out=alibi_cols[:], in0=alibi_ps[:], scalar1=SQRT_D, scalar2=None, op0=ALU.mult
+            out=alibi_cols[:], in0=alibi_ps[:].bitcast(BF16)[:, 0:P], scalar1=SQRT_D, scalar2=None, op0=ALU.mult
         )
         turn_queries_or_keys("q", 0)
         turn_queries_or_keys("k", 0)
@@ -424,20 +432,17 @@ def tile_fastbloomattention_pa_t_kernel(
                     scales=w_scales[:],
                     in_=w_grp[:].rearrange("p x t -> p (x t)"),
                 )
-            if k == 2 or k == 3:
-                quantise_hidden(0, 2 * (k - 2))
-                quantise_hidden(0, 2 * (k - 2) + 1)
-            if k == 3:
+            if 2 <= k < 6:
+                quantise_hidden(0, k - 2)
+            if k == 5:
                 load_hidden(1)
-            if 4 <= k < 8:
-                g, h = (k - 4) // 2, 2 * ((k - 4) % 2)
-                project_values(0, g, h)
-                project_values(0, g, h + 1)
+            if 4 <= k < 12:
+                project_values(0, (k - 4) // H, (k - 4) % H)
 
         def weighed_in(k):
-            if k == 8:
-                return 0
-            if k > 8 and k % ROWS == ROWS - 1 and k - 7 < ALL_ROWS:
+            if k == 12 or k == 13:
+                return k - 12
+            if k > 13 and k % ROWS == ROWS - 1 and k - 7 < ALL_ROWS:
                 return (k - 7) // ROWS
             return None
 
@@ -446,21 +451,19 @@ def tile_fastbloomattention_pa_t_kernel(
                 if k > 0 and k % ROWS == 0 and k // ROWS + AHEAD < ALL_CHUNKS:
                     build_term(k // ROWS + AHEAD)
                 multiply_keys(k)
-            done = weighed_in(k - 1)
-            if done is not None:
-                sum_rows(done)
+            if weighed_in(k - 1) is not None:
+                finish(weighed_in(k - 1))
             if k < ALL_ROWS:
                 add_term(k, 0)
-            if done is not None:
-                invert_sums(done)
-            if k < ALL_ROWS:
                 add_term(k, 1)
-            if done is not None:
-                finish(done)
-            if 0 <= k - 3 < ALL_ROWS:
-                quantise_e(k - 3)
+            if weighed_in(k + 1) is not None:
+                sum_rows(weighed_in(k + 1))
+            if weighed_in(k) is not None:
+                invert_sums(weighed_in(k))
             if k < ALL_ROWS:
                 find_shift(k)
+            if k % 2 == 0 and 0 <= k - 4 < ALL_ROWS:
+                quantise_e(k - 4)
             if 0 <= k - 2 < ALL_ROWS:
                 turn_e(k - 2)
             if 0 <= k - 1 < ALL_ROWS:

@@ -48,7 +48,7 @@ def tile_fastbloomattention_pa_t_kernel(
         terms = pools.enter_context(tc.tile_pool(name="terms", bufs=AHEAD + 2))
         stage = pools.enter_context(tc.tile_pool(name="stage", bufs=2))
         per_row = pools.enter_context(tc.tile_pool(name="per_row", bufs=3))
-        per_chunk = pools.enter_context(tc.tile_pool(name="per_chunk", bufs=3))
+        per_chunk = pools.enter_context(tc.tile_pool(name="per_chunk", bufs=4))
         psum_scores = pools.enter_context(tc.psum_pool(name="psum_scores", bufs=4))
         psum_turn = pools.enter_context(tc.psum_pool(name="psum_turn", bufs=4))
 
@@ -64,6 +64,7 @@ def tile_fastbloomattention_pa_t_kernel(
         term, scores, tops, shift, e, eT, e_grouped = {}, {}, {}, {}, {}, {}, {}
         e_quantised, part_sums, context_ps = {}, {}, {}
         sums, inverse = {}, {}
+        waiting = []
 
         def load_queries_and_keys(n):
             q_raw = per_head.tile([P, TILES, D], BF16)
@@ -82,7 +83,7 @@ def tile_fastbloomattention_pa_t_kernel(
                     turned_ps[:, t * P : (t + 1) * P], qk_raw[(label, n)][:, t, :], ident_bf[:]
                 )
             kept = per_head.tile([P, S], BF16, name=label + "T")
-            nc.scalar.copy(out=kept[:], in_=turned_ps[:])
+            nc.scalar.copy(out=kept[:].bitcast(F32), in_=turned_ps[:].bitcast(F32))
             qk_turned[(label, n)] = kept
 
         def load_mask(b, c):
@@ -110,14 +111,17 @@ def tile_fastbloomattention_pa_t_kernel(
         def keep_mask(b, piece, mask_ps, copy):
             c, j = piece // 4, piece % 4
             copy(
-                out=maskT[b][:, j, c * BANK : (c + 1) * BANK, :].rearrange("p i w -> p (i w)"),
-                in_=mask_ps[:].bitcast(BF16),
+                out=maskT[b][:, j, c * BANK : (c + 1) * BANK, :].rearrange("p i w -> p (i w)").bitcast(F32),
+                in_=mask_ps[:],
             )
 
-        def turn_mask(b, piece):
+        def turn_mask(b, piece, copy, wait=False):
             mask_ps = psum_turn.tile([P, BANK], F32, tag="turn")
             turn_mask_in_psum(b, piece, mask_ps)
-            keep_mask(b, piece, mask_ps, nc.vector.tensor_copy)
+            if wait:
+                waiting.append(lambda: keep_mask(b, piece, mask_ps, copy))
+            else:
+                keep_mask(b, piece, mask_ps, copy)
 
         def build_first_term():
             built = terms.tile([P, TILES, BANK], F32, name="term")
@@ -174,13 +178,12 @@ def tile_fastbloomattention_pa_t_kernel(
                     )
             hid_raw[b] = loaded
 
-        def quantise_hidden(b, j):
+        def turn_hidden(b, j):
             if j == 0:
                 h_quantised[b] = (
                     stage.tile([P, 4 * 2 * P], U32, align_bytes=64, name="h_codes"),
                     stage.tile([P, 4 * 2 * P], U8, align_bytes=64, name="h_scales"),
                 )
-            h_codes, h_scales = h_quantised[b]
             hid_words = hid_raw[b][:].bitcast(F32).rearrange("p (j s x) -> p j s x", j=4, s=2)
             hid_ps = psum_turn.tile([P, BANK], F32, tag="turn")
             for u in range(2):
@@ -189,7 +192,11 @@ def tile_fastbloomattention_pa_t_kernel(
                         nc, hid_ps, s * P, u, hid_words[:, j, s, u * P : (u + 1) * P], ident_f32[:]
                     )
             h_grp = stage.tile([P, 2 * P * 4], BF16, align_bytes=64)
-            nc.vector.tensor_copy(out=h_grp[:], in_=hid_ps[:].bitcast(BF16))
+            nc.scalar.copy(out=h_grp[:].bitcast(F32), in_=hid_ps[:])
+            waiting.append(lambda: quantise_hidden(b, j, h_grp))
+
+        def quantise_hidden(b, j, h_grp):
+            h_codes, h_scales = h_quantised[b]
             block = slice(j * 2 * P, (j + 1) * 2 * P)
             nc.vector.quantize_mx(
                 out=h_codes[:, block].bitcast(FP8X4), scales=h_scales[:, block], in_=h_grp[:]
@@ -202,7 +209,7 @@ def tile_fastbloomattention_pa_t_kernel(
                     per_batch.tile([P, PASSES * HD], U8, align_bytes=64, name="v_scales"),
                 )
             if h == 0:
-                v_grouped[b] = stage.tile([P, HD * 4], BF16, align_bytes=64, name="v_grp")
+                v_grouped[(b, g)] = stage.tile([P, HD * 4], BF16, align_bytes=64, name="v_grp")
             h_codes, h_scales = h_quantised[b]
             head = slice(h * D, (h + 1) * D)
             v_ps = psum_turn.tile([P, BANK], F32, tag="turn", name="v_ps")
@@ -217,20 +224,33 @@ def tile_fastbloomattention_pa_t_kernel(
                     start=True,
                     stop=True,
                 )
+            waiting.append(lambda: add_bias(b, g, h, v_ps))
+
+        def add_bias(b, g, h, v_ps):
+            head = slice(h * D, (h + 1) * D)
             nc.vector.tensor_tensor(
-                out=v_grouped[b][:, h * D * 4 : (h + 1) * D * 4].rearrange("p (d t) -> p d t", t=4),
+                out=v_grouped[(b, g)][:, h * D * 4 : (h + 1) * D * 4].rearrange("p (d t) -> p d t", t=4),
                 in0=v_ps[:].rearrange("p (t d) -> p d t", t=4),
                 in1=bias_bc[:, head].unsqueeze(2).to_broadcast([P, D, 4]),
                 op=ALU.add,
             )
             if h == H - 1:
-                v_codes, v_scales = v_quantised[b]
-                one_pass = slice(g * HD, (g + 1) * HD)
-                nc.vector.quantize_mx(
-                    out=v_codes[:, one_pass].bitcast(FP8X4),
-                    scales=v_scales[:, one_pass],
-                    in_=v_grouped[b][:],
-                )
+                waiting.append(lambda: quantise_values(b, g))
+
+        def quantise_values(b, g):
+            v_codes, v_scales = v_quantised[b]
+            one_pass = slice(g * HD, (g + 1) * HD)
+            nc.vector.quantize_mx(
+                out=v_codes[:, one_pass].bitcast(FP8X4),
+                scales=v_scales[:, one_pass],
+                in_=v_grouped[(b, g)][:],
+            )
+
+        def take_waiting_jobs():
+            jobs = list(waiting)
+            waiting.clear()
+            for job in jobs:
+                job()
 
         def prepare(n, i):
             b, h = n // H, n % H
@@ -249,9 +269,12 @@ def tile_fastbloomattention_pa_t_kernel(
         def prepare_values(n, i):
             b, h = n // H, n % H
             if b + 1 < B and h < 2 and i >= 4:
-                turn_mask(b + 1, 4 * h + i - 4)
-            if b + 1 < B and h >= 2 and 2 <= i < 4:
-                quantise_hidden(b + 1, 2 * (h - 2) + i - 2)
+                if i % 2 == 0:
+                    turn_mask(b + 1, 4 * h + i - 4, nc.vector.tensor_copy, wait=True)
+                else:
+                    turn_mask(b + 1, 4 * h + i - 4, nc.scalar.copy)
+            if b + 1 < B and 1 <= h < 3 and 2 <= i < 4:
+                turn_hidden(b + 1, 2 * (h - 1) + i - 2)
             if b + 1 < B and h >= 2 and i >= 4:
                 project_values(b + 1, h - 2, i - 4)
 
@@ -324,7 +347,7 @@ def tile_fastbloomattention_pa_t_kernel(
         def group_e(k):
             if k % 2 == 0:
                 e_grouped[k // 2] = per_row.tile([P, 2, S], BF16, align_bytes=64, name="e_grp")
-            nc.scalar.copy(out=e_grouped[k // 2][:, k % 2, :], in_=eT[k][:].bitcast(BF16))
+            nc.scalar.copy(out=e_grouped[k // 2][:, k % 2, :].bitcast(F32), in_=eT[k][:])
 
         def quantise_e(k):
             n, r = k // ROWS, k % ROWS
@@ -418,12 +441,12 @@ def tile_fastbloomattention_pa_t_kernel(
 
         def prepare_first_batch(k):
             if k == 0:
-                turn_mask(0, 4)
-                turn_mask(0, 5)
+                turn_mask(0, 4, nc.vector.tensor_copy)
+                turn_mask(0, 5, nc.scalar.copy)
                 nc.scalar.copy(out=w_grp[:], in_=w_raw[:].rearrange("p t x -> p x t"))
             if k == 1:
-                turn_mask(0, 6)
-                turn_mask(0, 7)
+                turn_mask(0, 6, nc.vector.tensor_copy)
+                turn_mask(0, 7, nc.scalar.copy)
                 build_term(1)
                 load_mask(1, 0)
                 load_mask(1, 1)
@@ -433,16 +456,16 @@ def tile_fastbloomattention_pa_t_kernel(
                     in_=w_grp[:].rearrange("p x t -> p (x t)"),
                 )
             if 2 <= k < 6:
-                quantise_hidden(0, k - 2)
+                turn_hidden(0, k - 2)
             if k == 5:
                 load_hidden(1)
-            if 4 <= k < 12:
-                project_values(0, (k - 4) // H, (k - 4) % H)
+            if 5 <= k < 13:
+                project_values(0, (k - 5) // H, (k - 5) % H)
 
         def weighed_in(k):
-            if k == 12 or k == 13:
-                return k - 12
-            if k > 13 and k % ROWS == ROWS - 1 and k - 7 < ALL_ROWS:
+            if 15 <= k < 18:
+                return k - 15
+            if k > 17 and k % ROWS == ROWS - 1 and k - 7 < ALL_ROWS:
                 return (k - 7) // ROWS
             return None
 
@@ -456,14 +479,18 @@ def tile_fastbloomattention_pa_t_kernel(
             if k < ALL_ROWS:
                 add_term(k, 0)
                 add_term(k, 1)
-            if weighed_in(k + 1) is not None:
-                sum_rows(weighed_in(k + 1))
+            if k % 2 == 0 and 0 <= k - 4 < ALL_ROWS:
+                quantise_e(k - 4)
+            if k % 2 == 1:
+                take_waiting_jobs()
+            if weighed_in(k + 2) is not None:
+                sum_rows(weighed_in(k + 2))
             if weighed_in(k) is not None:
                 invert_sums(weighed_in(k))
             if k < ALL_ROWS:
                 find_shift(k)
-            if k % 2 == 0 and 0 <= k - 4 < ALL_ROWS:
-                quantise_e(k - 4)
+            if k % 2 == 0:
+                take_waiting_jobs()
             if 0 <= k - 2 < ALL_ROWS:
                 turn_e(k - 2)
             if 0 <= k - 1 < ALL_ROWS:

import math
from contextlib import ExitStack

import concourse.mybir as mybir
from concourse.masks import make_identity

BF16 = mybir.dt.bfloat16
F32 = mybir.dt.float32
U32 = mybir.dt.uint32
U8 = mybir.dt.uint8
FP8X4 = mybir.dt.float8_e4m3fn_x4
ALU = mybir.AluOpType
ACT = mybir.ActivationFunctionType
AXIS = mybir.AxisListType

B, S, H, D = 4, 1024, 4, 128
HD = H * D
P = 128
TILES = S // P
BANK = 512
K_PASS = 512
PASSES = S // K_PASS
ROWS = 4
CHUNKS = TILES // ROWS
ALL_ROWS = B * H * TILES
ALL_CHUNKS = ALL_ROWS // ROWS
AHEAD = 2
SQRT_D = math.sqrt(D)

FLOPS = 2 * B * S * HD * HD + 2 * 2 * B * H * S * S * D


def turn_words(nc, bank, column, u, words, identity):
    nc.tensor.transpose(
        bank[:].rearrange("p (c u) -> p c u", u=2)[:, column : column + P, u], words, identity
    )


def tile_fastbloomattention_pa_t_kernel(
    tc, hidden_states, W_value, b_value, query, key, alibi, attention_mask, out
):
    nc = tc.nc
    with ExitStack() as pools:
        const = pools.enter_context(tc.tile_pool(name="const", bufs=1))
        raw = pools.enter_context(tc.tile_pool(name="raw", bufs=1))
        per_batch = pools.enter_context(tc.tile_pool(name="per_batch", bufs=2))
        per_head = pools.enter_context(tc.tile_pool(name="per_head", bufs=2))
        terms = pools.enter_context(tc.tile_pool(name="terms", bufs=AHEAD + 2))
        stage = pools.enter_context(tc.tile_pool(name="stage", bufs=2))
        per_row = pools.enter_context(tc.tile_pool(name="per_row", bufs=3))
        per_chunk = pools.enter_context(tc.tile_pool(name="per_chunk", bufs=4))
        psum_scores = pools.enter_context(tc.psum_pool(name="psum_scores", bufs=4))
        psum_turn = pools.enter_context(tc.psum_pool(name="psum_turn", bufs=4))

        ident_bf = const.tile([P, P], BF16)
        make_identity(nc, ident_bf[:])
        ident_f32 = const.tile([P, P], F32)
        make_identity(nc, ident_f32[:])
        pools.enter_context(tc.manual_schedule())

        qk_raw, qk_turned = {}, {}
        mask_raw, maskT, hid_raw = {}, {}, {}
        h_quantised, v_grouped, v_quantised = {}, {}, {}
        term, scores, tops, shift, e, eT, e_grouped = {}, {}, {}, {}, {}, {}, {}
        e_quantised, part_sums, context_ps = {}, {}, {}
        sums, inverse = {}, {}
        waiting = []

        def load_queries_and_keys(n):
            q_raw = per_head.tile([P, TILES, D], BF16)
            nc.sync.dma_start(out=q_raw[:], in_=query[n // H, n % H].rearrange("(t p) d -> p t d", p=P))
            k_raw = per_head.tile([P, TILES, D], BF16)
            nc.sync.dma_start(
                out=k_raw[:].rearrange("p (j w) d -> p j (w d)", w=2),
                in_=key[n // H, n % H].rearrange("(j p w) d -> p j (w d)", p=P, w=2),
            )
            qk_raw[("q", n)], qk_raw[("k", n)] = q_raw, k_raw

        def turn_queries_or_keys(label, n):
            turned_ps = psum_turn.tile([P, S], BF16, tag="turn", name=label + "_ps")
            for t in range(TILES):
                nc.tensor.transpose(
                    turned_ps[:, t * P : (t + 1) * P], qk_raw[(label, n)][:, t, :], ident_bf[:]
                )
            kept = per_head.tile([P, S], BF16, name=label + "T")
            nc.scalar.copy(out=kept[:].bitcast(F32), in_=turned_ps[:].bitcast(F32))
            qk_turned[(label, n)] = kept

        def load_mask(b, c):
            if c == 0:
                mask_raw[b] = raw.tile([P, TILES, S], BF16, name="mask_raw")
            its = slice(c * ROWS, (c + 1) * ROWS)
            nc.sync.dma_start(
                out=mask_raw[b][:, its, :],
                in_=attention_mask[b, 0].rearrange("(t p) k -> p t k", p=P)[:, its, :],
            )

        def turn_mask_in_psum(b, piece, mask_ps):
            c, j = piece // 4, piece % 4
            if piece == 0:
                maskT[b] = per_batch.tile([P, 4, S, 2], BF16, name="maskT")
            words = mask_raw[b][:].rearrange("p t k -> p (t k)").bitcast(F32)
            words = words.rearrange("p (t x) -> p t x", t=TILES)
            for r in range(ROWS):
                nc.tensor.transpose(
                    mask_ps[:, r * P : (r + 1) * P],
                    words[:, c * ROWS + r, j * P : (j + 1) * P],
                    ident_f32[:],
                )

        def keep_mask(b, piece, mask_ps, copy):
            c, j = piece // 4, piece % 4
            copy(
                out=maskT[b][:, j, c * BANK : (c + 1) * BANK, :].rearrange("p i w -> p (i w)").bitcast(F32),
                in_=mask_ps[:],
            )

        def turn_mask(b, piece, copy, wait=False):
            mask_ps = psum_turn.tile([P, BANK], F32, tag="turn")
            turn_mask_in_psum(b, piece, mask_ps)
            if wait:
                waiting.append(lambda: keep_mask(b, piece, mask_ps, copy))
            else:
                keep_mask(b, piece, mask_ps, copy)

        def build_first_term():
            built = terms.tile([P, TILES, BANK], F32, name="term")
            for piece in range(4):
                mask_ps = psum_scores.tile([P, BANK], F32, tag="scores")
                turn_mask_in_psum(0, piece, mask_ps)
                for w in range(2):
                    kt = 2 * piece + w
                    turned = mask_ps[:].bitcast(BF16).rearrange("p (i w) -> p i w", w=2)[:, :, w]
                    if piece % 2 == 0:
                        nc.vector.tensor_scalar(
                            out=built[:, kt, :],
                            in0=turned,
                            scalar1=SQRT_D,
                            scalar2=alibi_cols[:, kt : kt + 1],
                            op0=ALU.mult,
                            op1=ALU.add,
                        )
                    else:
                        nc.scalar.activation(
                            out=built[:, kt, :],
                            in_=turned,
                            func=ACT.Identity,
                            bias=alibi_cols[:, kt : kt + 1],
                            scale=SQRT_D,
                        )
                keep_mask(0, piece, mask_ps, nc.vector.tensor_copy if piece % 2 == 0 else nc.scalar.copy)
            term[0] = built

        def build_term(n):
            head, c = n // CHUNKS, n % CHUNKS
            built = terms.tile([P, TILES, BANK], F32, name="term")
            for kt in range(TILES):
                column = head * TILES + kt
                nc.gpsimd.tensor_scalar(
                    out=built[:, kt, :],
                    in0=maskT[head // H][:, kt // 2, c * BANK : (c + 1) * BANK, kt % 2],
                    scalar1=SQRT_D,
                    scalar2=alibi_cols[:, column : column + 1],
                    op0=ALU.mult,
                    op1=ALU.add,
                )
            term[n] = built

        def load_hidden(b):
            loaded = raw.tile([P, 4 * 2 * HD], BF16, name="hid_raw")
            for a in range(2):
                for s in range(2):
                    nc.sync.dma_start(
                        out=loaded[a * P // 2 : (a + 1) * P // 2, :].rearrange(
                            "y (j s c) -> y j s c", j=4, s=2
                        )[:, :, s, :],
                        in_=hidden_states[b].rearrange("(j y s a) c -> a s y j c", j=4, s=2, a=2)[a, s],
                    )
            hid_raw[b] = loaded

        def turn_hidden(b, j):
            if j == 0:
                h_quantised[b] = (
                    stage.tile([P, 4 * 2 * P], U32, align_bytes=64, name="h_codes"),
                    stage.tile([P, 4 * 2 * P], U8, align_bytes=64, name="h_scales"),
                )
            hid_words = hid_raw[b][:].bitcast(F32).rearrange("p (j s x) -> p j s x", j=4, s=2)
            hid_ps = psum_turn.tile([P, BANK], F32, tag="turn")
            for u in range(2):
                for s in range(2):
                    turn_words(
                        nc, hid_ps, s * P, u, hid_words[:, j, s, u * P : (u + 1) * P], ident_f32[:]
                    )
            h_grp = stage.tile([P, 2 * P * 4], BF16, align_bytes=64)
            nc.scalar.copy(out=h_grp[:].bitcast(F32), in_=hid_ps[:])
            waiting.append(lambda: quantise_hidden(b, j, h_grp))

        def quantise_hidden(b, j, h_grp):
            h_codes, h_scales = h_quantised[b]
            block = slice(j * 2 * P, (j + 1) * 2 * P)
            nc.vector.quantize_mx(
                out=h_codes[:, block].bitcast(FP8X4), scales=h_scales[:, block], in_=h_grp[:]
            )

        def project_values(b, g, h):
            if (g, h) == (0, 0):
                v_quantised[b] = (
                    per_batch.tile([P, PASSES * HD], U32, align_bytes=64, name="v_codes"),
                    per_batch.tile([P, PASSES * HD], U8, align_bytes=64, name="v_scales"),
                )
            if h == 0:
                v_grouped[(b, g)] = stage.tile([P, HD * 4], BF16, align_bytes=64, name="v_grp")
            h_codes, h_scales = h_quantised[b]
            head = slice(h * D, (h + 1) * D)
            v_ps = psum_turn.tile([P, BANK], F32, tag="turn", name="v_ps")
            for t in range(4):
                keys = slice((4 * g + t) * P, (4 * g + t + 1) * P)
                nc.tensor.matmul_mx(
                    out=v_ps[:, t * D : (t + 1) * D],
                    lhsT=h_codes[:, keys].bitcast(FP8X4),
                    lhsT_scale=h_scales[:, keys],
                    rhs=w_codes[:, head].bitcast(FP8X4),
                    rhs_scale=w_scales[:, head],
                    start=True,
                    stop=True,
                )
            waiting.append(lambda: add_bias(b, g, h, v_ps))

        def add_bias(b, g, h, v_ps):
            head = slice(h * D, (h + 1) * D)
            nc.vector.tensor_tensor(
                out=v_grouped[(b, g)][:, h * D * 4 : (h + 1) * D * 4].rearrange("p (d t) -> p d t", t=4),
                in0=v_ps[:].rearrange("p (t d) -> p d t", t=4),
                in1=bias_bc[:, head].unsqueeze(2).to_broadcast([P, D, 4]),
                op=ALU.add,
            )
            if h == H - 1:
                waiting.append(lambda: quantise_values(b, g))

        def quantise_values(b, g):
            v_codes, v_scales = v_quantised[b]
            one_pass = slice(g * HD, (g + 1) * HD)
            nc.vector.quantize_mx(
                out=v_codes[:, one_pass].bitcast(FP8X4),
                scales=v_scales[:, one_pass],
                in_=v_grouped[(b, g)][:],
            )

        def take_waiting_jobs():
            jobs = list(waiting)
            waiting.clear()
            for job in jobs:
                job()

        def prepare(n, i):
            b, h = n // H, n % H
            if i < 2 and n + 1 < B * H:
                turn_queries_or_keys("qk"[i], n + 1)
            if i == 2 and n + 2 < B * H:
                load_queries_and_keys(n + 2)
            if b + 1 >= B:
                return
            if h == 2 and i == 0 and b + 2 < B:
                load_mask(b + 2, 0)
                load_mask(b + 2, 1)
            if h == 3 and i == 7 and b + 2 < B:
                load_hidden(b + 2)

        def prepare_values(n, i):
            b, h = n // H, n % H
            if b + 1 < B and h < 2 and i >= 4:
                if i % 2 == 0:
                    turn_mask(b + 1, 4 * h + i - 4, nc.vector.tensor_copy, wait=True)
                else:
                    turn_mask(b + 1, 4 * h + i - 4, nc.scalar.copy)
            if b + 1 < B and 1 <= h < 3 and 2 <= i < 4:
                turn_hidden(b + 1, 2 * (h - 1) + i - 2)
            if b + 1 < B and h >= 2 and i >= 4:
                project_values(b + 1, h - 2, i - 4)

        def multiply_keys(k):
            queries = slice((k % TILES) * P, (k % TILES + 1) * P)
            for half in range(2):
                scores[(k, half)] = psum_scores.tile([P, BANK], F32, tag="scores", name="bank")
                nc.tensor.matmul(
                    scores[(k, half)][:],
                    lhsT=qk_turned[("q", k // TILES)][:, queries],
                    rhs=qk_turned[("k", k // TILES)][:, half * BANK : (half + 1) * BANK],
                    start=True,
                    stop=False,
                )

        def add_term(k, half):
            n, r = k // ROWS, k % ROWS
            if half == 0:
                tops[k] = per_row.tile([P, 2], F32, name="tops")
            bank = scores[(k, half)]
            for a in range(4):
                nc.tensor.matmul(
                    bank[:, a * P : (a + 1) * P],
                    lhsT=term[n][:, 4 * half + a, r * P : (r + 1) * P],
                    rhs=ident_f32[:],
                    start=False,
                    stop=(a == 3),
                    is_transpose=True,
                )
            nc.vector.tensor_reduce(
                out=tops[k][:, half : half + 1], in_=bank[:], axis=AXIS.X, op=ALU.max
            )

        def find_shift(k):
            shift[k] = per_row.tile([P, 1], F32, name="shift")
            nc.vector.tensor_scalar(
                out=shift[k][:],
                in0=tops[k][:, 0:1],
                scalar1=tops[k][:, 1:2],
                scalar2=-1.0 / SQRT_D,
                op0=ALU.max,
                op1=ALU.mult,
            )

        def exponentials(k):
            n, r = k // ROWS, k % ROWS
            if r == 0:
                part_sums[n] = per_chunk.tile([P, ROWS, 2], F32, name="part_sums")
            e[k] = per_row.tile([P, S], BF16, name="e")
            for half in range(2):
                nc.scalar.activation(
                    out=e[k][:, half * BANK : (half + 1) * BANK],
                    in_=scores[(k, half)][:],
                    func=ACT.Exp,
                    bias=shift[k][:],
                    scale=1.0 / SQRT_D,
                    accum_out=part_sums[n][:, r, half : half + 1],
                )

        def turn_e(k):
            e_words = e[k][:].bitcast(F32)
            eT[k] = psum_turn.tile([P, BANK], F32, tag="turn", name="eT_ps")
            for g in range(PASSES):
                for u in range(2):
                    turn_words(
                        nc, eT[k], g * P, u, e_words[:, (2 * g + u) * P : (2 * g + u + 1) * P],
                        ident_f32[:],
                    )

        def group_e(k):
            if k % 2 == 0:
                e_grouped[k // 2] = per_row.tile([P, 2, S], BF16, align_bytes=64, name="e_grp")
            nc.scalar.copy(out=e_grouped[k // 2][:, k % 2, :].bitcast(F32), in_=eT[k][:])

        def quantise_e(k):
            n, r = k // ROWS, k % ROWS
            if r == 0:
                e_quantised[n] = (
                    per_chunk.tile([P, ROWS * PASSES * P], U32, align_bytes=64, name="e_codes"),
                    per_chunk.tile([P, ROWS * PASSES * P], U8, align_bytes=64, name="e_scales"),
                )
            e_codes, e_scales = e_quantised[n]
            ours = slice(r * PASSES * P, (r + 2) * PASSES * P)
            nc.vector.quantize_mx(
                out=e_codes[:, ours].bitcast(FP8X4),
                scales=e_scales[:, ours],
                in_=e_grouped[k // 2][:].rearrange("p a s -> p (a s)"),
            )

        def weigh_values(n):
            b, h = n // (H * CHUNKS), (n // CHUNKS) % H
            e_codes, e_scales = e_quantised[n]
            v_codes, v_scales = v_quantised[b]
            context_ps[n] = psum_turn.tile([P, BANK], F32, tag="turn", name="context_ps")
            for r in range(ROWS):
                for g in range(PASSES):
                    mine = slice((r * PASSES + g) * P, (r * PASSES + g + 1) * P)
                    theirs = slice(g * HD + h * D, g * HD + (h + 1) * D)
                    nc.tensor.matmul_mx(
                        out=context_ps[n][:, r * D : (r + 1) * D],
                        lhsT=e_codes[:, mine].bitcast(FP8X4),
                        lhsT_scale=e_scales[:, mine],
                        rhs=v_codes[:, theirs].bitcast(FP8X4),
                        rhs_scale=v_scales[:, theirs],
                        start=(g == 0),
                        stop=(g == PASSES - 1),
                    )

        def sum_rows(n):
            sums[n] = per_chunk.tile([P, ROWS], F32, name="sums")
            nc.vector.tensor_reduce(out=sums[n][:], in_=part_sums[n][:], axis=AXIS.X, op=ALU.add)

        def invert_sums(n):
            inverse[n] = per_chunk.tile([P, ROWS], F32, name="inverse")
            nc.vector.reciprocal(out=inverse[n][:], in_=sums[n][:])

        def finish(n):
            b, h, c = n // (H * CHUNKS), (n // CHUNKS) % H, n % CHUNKS
            context = per_chunk.tile([P, ROWS, D], F32)
            nc.vector.tensor_tensor(
                out=context[:],
                in0=context_ps[n][:].rearrange("p (r d) -> p r d", r=ROWS),
                in1=inverse[n][:].unsqueeze(2).to_broadcast([P, ROWS, D]),
                op=ALU.mult,
            )
            nc.sync.dma_start(
                out=out[b].rearrange("(t p) x -> p t x", p=P)[
                    :, c * ROWS : (c + 1) * ROWS, h * D : (h + 1) * D
                ],
                in_=context[:],
            )

        alibi_rows = const.tile([P, 2 * P], BF16)
        for half in range(2):
            nc.sync.dma_start(
                out=alibi_rows[half * P // 2 : (half + 1) * P // 2, :],
                in_=alibi.rearrange("b h o (j k) -> (b h o j) k", k=2 * P),
            )
        load_queries_and_keys(0)
        load_mask(0, 0)
        w_raw = const.tile([P, 4, HD], BF16)
        nc.sync.dma_start(
            out=w_raw[:].rearrange("p (u w) x -> p u (w x)", u=2),
            in_=W_value.rearrange("(u p w) x -> p u (w x)", u=2, w=2),
        )
        load_mask(0, 1)
        load_queries_and_keys(1)
        load_hidden(0)
        bias_bc = const.tile([P, HD], BF16)
        nc.sync.dma_start(out=bias_bc[:], in_=b_value.partition_broadcast(P))

        alibi_ps = psum_turn.tile([P, P], F32, tag="turn")
        nc.tensor.transpose(alibi_ps[:], alibi_rows[:].bitcast(F32), ident_f32[:])
        alibi_cols = const.tile([P, P], F32)
        nc.vector.tensor_scalar(
            out=alibi_cols[:], in0=alibi_ps[:].bitcast(BF16)[:, 0:P], scalar1=SQRT_D, scalar2=None, op0=ALU.mult
        )
        turn_queries_or_keys("q", 0)
        turn_queries_or_keys("k", 0)
        build_first_term()
        w_grp = const.tile([P, HD, 4], BF16, align_bytes=64)
        w_codes = const.tile([P, HD], U32, align_bytes=64)
        w_scales = const.tile([P, HD], U8, align_bytes=64)

        def prepare_first_batch(k):
            if k == 0:
                turn_mask(0, 4, nc.vector.tensor_copy)
                turn_mask(0, 5, nc.scalar.copy)
                nc.scalar.copy(out=w_grp[:], in_=w_raw[:].rearrange("p t x -> p x t"))
            if k == 1:
                turn_mask(0, 6, nc.vector.tensor_copy)
                turn_mask(0, 7, nc.scalar.copy)
                build_term(1)
                load_mask(1, 0)
                load_mask(1, 1)
                nc.vector.quantize_mx(
                    out=w_codes[:].bitcast(FP8X4),
                    scales=w_scales[:],
                    in_=w_grp[:].rearrange("p x t -> p (x t)"),
                )
            if 2 <= k < 6:
                turn_hidden(0, k - 2)
            if k == 5:
                load_hidden(1)
            if 5 <= k < 13:
                project_values(0, (k - 5) // H, (k - 5) % H)

        def weighed_in(k):
            if 15 <= k < 18:
                return k - 15
            if k > 17 and k % ROWS == ROWS - 1 and k - 7 < ALL_ROWS:
                return (k - 7) // ROWS
            return None

        for k in range(ALL_ROWS + 6):
            if k < ALL_ROWS:
                if k > 0 and k % ROWS == 0 and k // ROWS + AHEAD < ALL_CHUNKS:
                    build_term(k // ROWS + AHEAD)
                multiply_keys(k)
            if weighed_in(k - 1) is not None:
                finish(weighed_in(k - 1))
            if k < ALL_ROWS:
                add_term(k, 0)
                add_term(k, 1)
            if k % 2 == 0 and 0 <= k - 4 < ALL_ROWS:
                quantise_e(k - 4)
            if k % 2 == 1:
                take_waiting_jobs()
            if weighed_in(k + 2) is not None:
                sum_rows(weighed_in(k + 2))
            if weighed_in(k) is not None:
                invert_sums(weighed_in(k))
            if k < ALL_ROWS:
                find_shift(k)
            if k % 2 == 0:
                take_waiting_jobs()
            if 0 <= k - 2 < ALL_ROWS:
                turn_e(k - 2)
            if 0 <= k - 1 < ALL_ROWS:
                exponentials(k - 1)
            if 0 <= k - 2 < ALL_ROWS:
                group_e(k - 2)
            if k < ALL_ROWS:
                prepare_values(k // TILES, k % TILES)
            if weighed_in(k) is not None:
                weigh_values(weighed_in(k))
            if k < ALL_ROWS:
                prepare_first_batch(k)
                prepare(k // TILES, k % TILES)
            if k == 2:
                build_term(2)
